import numpy as np
import ml_dtypes


def mxq(x, axis, fmt="e4m3"):
    dtype, down = {"e4m3": (ml_dtypes.float8_e4m3fn, 7), "e5m2": (ml_dtypes.float8_e5m2, 14)}[fmt]
    v = np.moveaxis(np.asarray(x, np.float32).astype(ml_dtypes.bfloat16).astype(np.float64), axis, -1)
    blocks = v.reshape(v.shape[:-1] + (-1, 32))
    amax = np.abs(blocks).max(-1, keepdims=True)
    byte = np.maximum(np.where(amax > 0, np.frexp(amax)[1] - 1 + 127, 0) - down, 1)
    scale = np.exp2(byte - 127.0)
    codes = (blocks / scale).astype(np.float32).astype(dtype).astype(np.float64)
    return np.moveaxis((codes * scale).reshape(v.shape), -1, axis)


WIDE = False


def mx_kscale(k):
    if not WIDE:
        return np.ones(k)
    levels = np.array([10, -10, 5, -5, 0])
    a = np.random.permutation(np.resize(levels, k // 512 * 4)).reshape(k // 512, 4)
    idx = np.arange(k)
    return np.exp2(a[idx // 512, idx % 128 // 32])


BF16 = ml_dtypes.bfloat16


def bf(x):
    return np.asarray(x, np.float32).astype(BF16)


def f64(x):
    return np.asarray(x).astype(np.float64)


B, N, DIN, DH, DOUT = 64, 2, 512, 512, 512
EPS = 1e-5


def elu(v):
    return np.where(v > 0.0, v, np.expm1(np.minimum(v, 0.0)))


def sigmoid(v):
    return 1.0 / (1.0 + np.exp(-v))


def setup_inputs():
    rn = np.random.standard_normal
    s, t = mx_kscale(DH), mx_kscale(DOUT)
    z = rn((B, N, DOUT))
    e = np.exp(z - z.max(1, keepdims=True))
    return {
        "hv": bf(elu(rn((B, N, DH))) * s),
        "x": bf(rn((B, N, DIN)) + 0.5),
        "sel_w": bf(e / e.sum(1, keepdims=True)),
        "vW1": bf(rn((N, DH, DOUT)) * 1.2 / np.sqrt(DH) / s[:, None] * t),
        "vb1": bf(rn((N, DOUT)) * 0.3 * t),
        "vW4": bf(rn((N, DOUT, DOUT)) / np.sqrt(DOUT) / t[:, None]),
        "vb4": bf(rn((N, DOUT)) * 0.3),
        "vW5": bf(rn((N, DOUT, DOUT)) / np.sqrt(DOUT) / t[:, None]),
        "vb5": bf(rn((N, DOUT)) * 0.3),
        "vlng": bf(1.0 + 0.2 * rn((N, DOUT))),
        "vlnb": bf(0.2 * rn((N, DOUT))),
    }


def reference(hv, x, sel_w, vW1, vb1, vW4, vb4, vW5, vb5, vlng, vlnb):
    hq = mxq(f64(hv).transpose(1, 0, 2), 2, "e4m3")
    e1v = (hq @ mxq(f64(vW1), 1, "e4m3")) + f64(vb1)[:, None, :]
    eq = mxq(e1v, 2, "e4m3")
    gv = sigmoid((eq @ mxq(f64(vW4), 1, "e4m3")) + f64(vb4)[:, None, :]) * ((eq @ mxq(f64(vW5), 1, "e4m3")) + f64(vb5)[:, None, :])
    r = f64(x) + gv.transpose(1, 0, 2)
    yv = (r - r.mean(-1, keepdims=True)) * (1.0 / np.sqrt(r.var(-1, keepdims=True) + EPS)) * f64(vlng) + f64(vlnb)
    return np.sum(f64(sel_w) * yv, axis=1)

@@ -1,0 +1,274 @@
+from contextlib import ExitStack
+
+import concourse.mybir as mybir
+from concourse.masks import make_identity
+
+F32 = mybir.dt.float32
+BF16 = mybir.dt.bfloat16
+U32 = mybir.dt.uint32
+U8 = mybir.dt.uint8
+FP8X4 = mybir.dt.float8_e4m3fn_x4
+ALU = mybir.AluOpType
+ACT = mybir.ActivationFunctionType
+
+P = 128
+PACK = 4
+BATCH = 64
+VARS = 2
+FEAT = 512
+CHUNKS = FEAT // P
+HALVES = P // BATCH
+PAIRS = CHUNKS // HALVES
+EPS = 1e-5
+FLOPS = 2 * 3 * VARS * BATCH * FEAT * FEAT
+
+SCALAR_COLS = 384
+RUN = 4
+VB1 = 0
+VB4 = 1
+VB5 = 2
+GAIN = 3
+SHIFT = 4
+
+
+def load_weight(nc, pool, weight, label):
+    raw = pool.tile([P, PACK, FEAT], BF16, name="raw_%s" % label)
+    nc.sync.dma_start(out=raw[:], in_=weight.rearrange("(t p) c -> p t c", p=P))
+    return raw
+
+
+def quantise_weight(nc, pool, raw, label):
+    grouped = pool.tile([P, FEAT, PACK], BF16, name="grouped_%s" % label, align_bytes=64)
+    source = raw[:].rearrange("p t (c i) -> p c t i", i=RUN)
+    target = grouped[:].rearrange("p (c i) t -> p c t i", i=RUN)
+    split = SCALAR_COLS // RUN
+    nc.scalar.copy(out=target[:, :split], in_=source[:, :split])
+    nc.vector.tensor_copy(out=target[:, split:], in_=source[:, split:])
+    codes = pool.tile([P, FEAT], U32, name="codes_%s" % label, align_bytes=64)
+    scales = pool.tile([P, FEAT], U8, name="scales_%s" % label, align_bytes=64)
+    nc.vector.quantize_mx(
+        out=codes[:].bitcast(FP8X4),
+        scales=scales[:],
+        in_=grouped[:].rearrange("p c t -> p (c t)"),
+    )
+    return codes, scales
+
+
+def weight_times_batch(nc, acc, weight, moving):
+    codes, scales = weight
+    moving_codes, moving_scales = moving
+    for c in range(CHUNKS):
+        cols = slice(c * P, (c + 1) * P)
+        nc.tensor.matmul_mx(
+            out=acc[:, c, :],
+            lhsT=codes[:, cols].bitcast(FP8X4),
+            lhsT_scale=scales[:, cols],
+            rhs=moving_codes.bitcast(FP8X4),
+            rhs_scale=moving_scales,
+            start=True,
+            stop=True,
+        )
+
+
+def to_rows(nc, rows, by_feature, identity):
+    for j in range(PAIRS):
+        chunk_pair = by_feature[:, j * HALVES : (j + 1) * HALVES, :]
+        nc.tensor.transpose(rows[:, j, :], chunk_pair.rearrange("p h b -> p (h b)"), identity[:])
+
+
+def tile_variableselectionnetwork_pb_s_kernel(
+    tc, hv, x, sel_w, vW1, vb1, vW4, vb4, vW5, vb5, vlng, vlnb, out
+):
+    nc = tc.nc
+    with ExitStack() as stack:
+        keep = stack.enter_context(tc.tile_pool(name="keep", bufs=1))
+        short_ps = stack.enter_context(tc.psum_pool(name="short_ps", bufs=2))
+        acc_ps = stack.enter_context(tc.psum_pool(name="acc_ps", bufs=3))
+        rows_ps = stack.enter_context(tc.psum_pool(name="rows_ps", bufs=1))
+        keep_ps = stack.enter_context(tc.psum_pool(name="keep_ps", bufs=1))
+
+        ident_bf = keep.tile([P, P], BF16)
+        make_identity(nc, ident_bf[:])
+        ident_f = keep.tile([P, P], F32)
+        make_identity(nc, ident_f[:])
+        minus_half = keep.tile([P, 1], F32)
+        nc.vector.memset(minus_half[:], -0.5)
+        table_warm = keep.tile([P, 1], F32)
+        nc.scalar.activation(out=table_warm[:], in_=minus_half[:], func=ACT.Sigmoid)
+        vec_rows = keep.tile([P, FEAT], BF16)
+        nc.vector.memset(vec_rows[:], 0.0)
+
+        hv_sb = keep.tile([P, FEAT], BF16)
+        nc.sync.dma_start(out=hv_sb[:], in_=hv.rearrange("b n k -> (b n) k"))
+        vectors = {VB1: vb1, VB4: vb4, VB5: vb5, GAIN: vlng, SHIFT: vlnb}
+        for place, vector in vectors.items():
+            nc.scalar.dma_start(out=vec_rows[VARS * place : VARS * (place + 1), :], in_=vector)
+        sel_sb = keep.tile([P, FEAT], BF16)
+        nc.sync.dma_start(out=sel_sb[:], in_=sel_w.rearrange("b n f -> (b n) f"))
+        raw1 = [load_weight(nc, keep, vW1[n, :, :], "w1_%d" % n) for n in range(VARS)]
+        raw4 = [load_weight(nc, keep, vW4[n, :, :], "w4_%d" % n) for n in range(VARS)]
+        raw5 = [load_weight(nc, keep, vW5[n, :, :], "w5_%d" % n) for n in range(VARS)]
+        x_rows = keep.tile([P, VARS, PAIRS, P], BF16)
+        x_halves = x.rearrange("b n (j h q) -> h b n j q", h=HALVES, q=P)
+        for h in range(HALVES):
+            nc.gpsimd.dma_start(out=x_rows[h * BATCH : (h + 1) * BATCH], in_=x_halves[h])
+
+        hv_t = short_ps.tile([P, PACK, P], BF16, tag="short")
+        for t in range(PACK):
+            nc.tensor.transpose(hv_t[:, t, :], hv_sb[:, t * P : (t + 1) * P], ident_bf[:])
+        hv_grouped = keep.tile([P, VARS, BATCH, PACK], BF16, align_bytes=64)
+        nc.scalar.copy(out=hv_grouped[:], in_=hv_t[:].rearrange("p t (b n) -> p n b t", n=VARS))
+        hv_codes = keep.tile([P, VARS, BATCH], U32, align_bytes=64)
+        hv_scales = keep.tile([P, VARS, BATCH], U8, align_bytes=64)
+        nc.vector.quantize_mx(
+            out=hv_codes[:].rearrange("p n b -> p (n b)").bitcast(FP8X4),
+            scales=hv_scales[:].rearrange("p n b -> p (n b)"),
+            in_=hv_grouped[:].rearrange("p n b t -> p (n b t)"),
+        )
+
+        vec_t = short_ps.tile([P, CHUNKS, P], BF16, tag="short")
+        for c in range(CHUNKS):
+            nc.tensor.transpose(vec_t[:, c, :], vec_rows[:, c * P : (c + 1) * P], ident_bf[:])
+        vecs = keep.tile([P, len(vectors) * VARS, CHUNKS], F32)
+        nc.vector.tensor_copy(
+            out=vecs[:], in_=vec_t[:, :, : len(vectors) * VARS].rearrange("p c r -> p r c")
+        )
+
+        def per_feature(vector, n):
+            return vecs[:, VARS * vector + n, :]
+
+        def along_batch(vector, n):
+            return per_feature(vector, n).unsqueeze(2).to_broadcast([P, CHUNKS, BATCH])
+
+        sel_t = short_ps.tile([P, CHUNKS, P], BF16, tag="short")
+        for c in range(CHUNKS):
+            nc.tensor.transpose(sel_t[:, c, :], sel_sb[:, c * P : (c + 1) * P], ident_bf[:])
+        sel_by_var = sel_t[:].rearrange("p c (b n) -> p n c b", n=VARS)
+        gain_rows = keep_ps.tile([P, VARS, PAIRS, P], F32)
+        shifted = []
+        for n in range(VARS):
+            sel_gain = keep.tile([P, CHUNKS, BATCH], F32, name="sel_gain_%d" % n)
+            nc.vector.tensor_tensor(
+                out=sel_gain[:], in0=sel_by_var[:, n], in1=along_batch(GAIN, n), op=ALU.mult
+            )
+            to_rows(nc, gain_rows[:, n], sel_gain, ident_f)
+            sel_shift = keep.tile([P, CHUNKS, BATCH], F32, name="sel_shift_%d" % n)
+            nc.vector.tensor_tensor(
+                out=sel_shift[:], in0=sel_by_var[:, n], in1=along_batch(SHIFT, n), op=ALU.mult
+            )
+            shifted.append(sel_shift)
+        shift_sum = keep.tile([P, CHUNKS, BATCH], F32)
+        nc.vector.tensor_tensor(out=shift_sum[:], in0=shifted[0][:], in1=shifted[1][:], op=ALU.add)
+        shift_rows = keep_ps.tile([P, PAIRS, P], F32)
+        to_rows(nc, shift_rows, shift_sum, ident_f)
+
+        pair = keep.tile([P, HALVES, BATCH], F32)
+        nc.vector.tensor_tensor(
+            out=pair[:],
+            in0=ident_f[:, :BATCH].unsqueeze(1).to_broadcast([P, HALVES, BATCH]),
+            in1=ident_f[:, BATCH:].unsqueeze(1).to_broadcast([P, HALVES, BATCH]),
+            op=ALU.add,
+        )
+
+        e1_codes = keep.tile([P, VARS, BATCH], U32, align_bytes=64)
+        e1_scales = keep.tile([P, VARS, BATCH], U8, align_bytes=64)
+        for n in range(VARS):
+            w1 = quantise_weight(nc, keep, raw1[n], "w1_%d" % n)
+            e1_acc = acc_ps.tile([P, CHUNKS, BATCH], F32, tag="acc")
+            weight_times_batch(nc, e1_acc, w1, (hv_codes[:, n, :], hv_scales[:, n, :]))
+            e1_grouped = keep.tile([P, BATCH, PACK], BF16, name="e1_grouped_%d" % n, align_bytes=64)
+            nc.vector.tensor_tensor(
+                out=e1_grouped[:],
+                in0=e1_acc[:].rearrange("p c b -> p b c"),
+                in1=per_feature(VB1, n).unsqueeze(1).to_broadcast([P, BATCH, PACK]),
+                op=ALU.add,
+            )
+            nc.vector.quantize_mx(
+                out=e1_codes[:, n, :].bitcast(FP8X4),
+                scales=e1_scales[:, n, :],
+                in_=e1_grouped[:].rearrange("p b c -> p (b c)"),
+            )
+
+        gates = []
+        for n in range(VARS):
+            w4 = quantise_weight(nc, keep, raw4[n], "w4_%d" % n)
+            gate_acc = acc_ps.tile([P, CHUNKS, BATCH], F32, tag="acc")
+            weight_times_batch(nc, gate_acc, w4, (e1_codes[:, n, :], e1_scales[:, n, :]))
+            gate = keep.tile([P, CHUNKS, BATCH], F32, name="gate_%d" % n)
+            for c in range(CHUNKS):
+                nc.scalar.activation(
+                    out=gate[:, c, :],
+                    in_=gate_acc[:, c, :],
+                    func=ACT.Sigmoid,
+                    bias=per_feature(VB4, n)[:, c : c + 1],
+                )
+            gates.append(gate)
+
+        total = shift_rows[:].rearrange("p j q -> p (j q)")
+        for n in range(VARS):
+            w5 = quantise_weight(nc, keep, raw5[n], "w5_%d" % n)
+            value_acc = acc_ps.tile([P, CHUNKS, BATCH], F32, tag="acc")
+            weight_times_batch(nc, value_acc, w5, (e1_codes[:, n, :], e1_scales[:, n, :]))
+            gv = keep.tile([P, CHUNKS, BATCH], F32, name="gv_%d" % n)
+            for c in range(CHUNKS):
+                nc.vector.scalar_tensor_tensor(
+                    out=gv[:, c, :],
+                    in0=value_acc[:, c, :],
+                    scalar=per_feature(VB5, n)[:, c : c + 1],
+                    in1=gates[n][:, c, :],
+                    op0=ALU.add,
+                    op1=ALU.mult,
+                )
+            gv_rows = rows_ps.tile([P, PAIRS, P], F32, tag="rows")
+            to_rows(nc, gv_rows, gv, ident_f)
+            resid = keep.tile([P, PAIRS * P], F32, name="resid_%d" % n)
+            nc.vector.tensor_tensor(
+                out=resid[:],
+                in0=gv_rows[:].rearrange("p j q -> p (j q)"),
+                in1=x_rows[:, n].rearrange("p j q -> p (j q)"),
+                op=ALU.add,
+            )
+
+            stats = keep.tile([P, 6], F32, name="stats_%d" % n)
+            nc.vector.bn_stats(out=stats[:], in_=resid[:])
+            own = keep.tile([P, 2], F32, name="own_%d" % n)
+            nc.vector.bn_aggr(out=own[:], in_=stats[:])
+            sums = short_ps.tile([P, 2], F32, tag="short")
+            nc.tensor.matmul(
+                out=sums[:], lhsT=pair[:].rearrange("p h b -> p (h b)"), rhs=own[:], start=True, stop=True
+            )
+            avg = keep.tile([P, 2], F32, name="avg_%d" % n)
+            nc.vector.tensor_scalar(
+                out=avg[:], in0=sums[:], scalar1=1.0 / HALVES, scalar2=None, op0=ALU.mult
+            )
+            mean = avg[:, 0:1]
+            dev = keep.tile([P, 1], F32, name="dev_%d" % n)
+            nc.vector.tensor_tensor(out=dev[:], in0=own[:, 0:1], in1=mean, op=ALU.subtract)
+            dev_sq = keep.tile([P, 1], F32, name="dev_sq_%d" % n)
+            nc.vector.tensor_scalar(
+                out=dev_sq[:], in0=dev[:], scalar1=dev[:], scalar2=EPS, op0=ALU.mult, op1=ALU.add
+            )
+            var_eps = keep.tile([P, 1], F32, name="var_eps_%d" % n)
+            nc.vector.tensor_tensor(out=var_eps[:], in0=dev_sq[:], in1=avg[:, 1:2], op=ALU.add)
+            rstd = keep.tile([P, 1], F32, name="rstd_%d" % n)
+            nc.gpsimd.tensor_tensor(out=rstd[:], in0=var_eps[:], in1=minus_half[:], op=ALU.pow)
+
+            weighted = keep.tile([P, PAIRS * P], F32, name="weighted_%d" % n)
+            nc.vector.scalar_tensor_tensor(
+                out=weighted[:],
+                in0=resid[:],
+                scalar=mean,
+                in1=gain_rows[:, n].rearrange("p j q -> p (j q)"),
+                op0=ALU.subtract,
+                op1=ALU.mult,
+            )
+            summed = keep.tile([P, PAIRS * P], F32, name="summed_%d" % n)
+            nc.vector.scalar_tensor_tensor(
+                out=summed[:], in0=weighted[:], scalar=rstd[:], in1=total, op0=ALU.mult, op1=ALU.add
+            )
+            total = summed[:]
+
+        out_halves = out.rearrange("b (j h q) -> h b j q", h=HALVES, q=P)
+        result = total.rearrange("p (j q) -> p j q", q=P)
+        nc.sync.dma_start(out=out_halves[0], in_=result[:BATCH])
+        nc.scalar.dma_start(out=out_halves[1], in_=result[BATCH:])

@@ -22,7 +22,7 @@ PAIRS = CHUNKS // HALVES
 EPS = 1e-5
 FLOPS = 2 * 3 * VARS * BATCH * FEAT * FEAT
 
-SCALAR_COLS = 384
+SCALAR_COLS = 256
 RUN = 4
 VB1 = 0
 VB4 = 1
@@ -37,13 +37,17 @@ def load_weight(nc, pool, weight, label):
     return raw
 
 
-def quantise_weight(nc, pool, raw, label):
+def regroup(nc, pool, raw, label):
     grouped = pool.tile([P, FEAT, PACK], BF16, name="grouped_%s" % label, align_bytes=64)
     source = raw[:].rearrange("p t (c i) -> p c t i", i=RUN)
     target = grouped[:].rearrange("p (c i) t -> p c t i", i=RUN)
     split = SCALAR_COLS // RUN
     nc.scalar.copy(out=target[:, :split], in_=source[:, :split])
     nc.vector.tensor_copy(out=target[:, split:], in_=source[:, split:])
+    return grouped
+
+
+def quantise(nc, pool, grouped, label):
     codes = pool.tile([P, FEAT], U32, name="codes_%s" % label, align_bytes=64)
     scales = pool.tile([P, FEAT], U8, name="scales_%s" % label, align_bytes=64)
     nc.vector.quantize_mx(
@@ -54,9 +58,8 @@ def quantise_weight(nc, pool, raw, label):
     return codes, scales
 
 
-def weight_times_batch(nc, acc, weight, moving):
+def multiply(nc, acc, weight, moving_codes, moving_scales):
     codes, scales = weight
-    moving_codes, moving_scales = moving
     for c in range(CHUNKS):
         cols = slice(c * P, (c + 1) * P)
         nc.tensor.matmul_mx(
@@ -83,20 +86,23 @@ def tile_variableselectionnetwork_pb_s_kernel(
     with ExitStack() as stack:
         keep = stack.enter_context(tc.tile_pool(name="keep", bufs=1))
         short_ps = stack.enter_context(tc.psum_pool(name="short_ps", bufs=2))
-        acc_ps = stack.enter_context(tc.psum_pool(name="acc_ps", bufs=3))
-        rows_ps = stack.enter_context(tc.psum_pool(name="rows_ps", bufs=1))
+        acc_ps = stack.enter_context(tc.psum_pool(name="acc_ps", bufs=2))
+        rows_ps = stack.enter_context(tc.psum_pool(name="rows_ps", bufs=2))
         keep_ps = stack.enter_context(tc.psum_pool(name="keep_ps", bufs=1))
+        stack.enter_context(tc.manual_schedule())
 
-        ident_bf = keep.tile([P, P], BF16)
-        make_identity(nc, ident_bf[:])
-        ident_f = keep.tile([P, P], F32)
-        make_identity(nc, ident_f[:])
-        minus_half = keep.tile([P, 1], F32)
-        nc.vector.memset(minus_half[:], -0.5)
-        table_warm = keep.tile([P, 1], F32)
-        nc.scalar.activation(out=table_warm[:], in_=minus_half[:], func=ACT.Sigmoid)
         vec_rows = keep.tile([P, FEAT], BF16)
         nc.vector.memset(vec_rows[:], 0.0)
+        ident_bf = keep.tile([P, P], BF16)
+        nc.vector.memset(ident_bf[:], 0.0)
+        make_identity(nc, ident_bf[:], nomemset=True)
+        ident_f = keep.tile([P, P], F32)
+        nc.vector.memset(ident_f[:], 0.0)
+        make_identity(nc, ident_f[:], nomemset=True)
+        one = keep.tile([P, 1], F32)
+        nc.vector.memset(one[:], 1.0)
+        warm = keep.tile([P, 2], F32)
+        nc.scalar.activation(out=warm[:, 0:1], in_=one[:], func=ACT.Sigmoid)
 
         hv_sb = keep.tile([P, FEAT], BF16)
         nc.sync.dma_start(out=hv_sb[:], in_=hv.rearrange("b n k -> (b n) k"))
@@ -118,13 +124,6 @@ def tile_variableselectionnetwork_pb_s_kernel(
             nc.tensor.transpose(hv_t[:, t, :], hv_sb[:, t * P : (t + 1) * P], ident_bf[:])
         hv_grouped = keep.tile([P, VARS, BATCH, PACK], BF16, align_bytes=64)
         nc.scalar.copy(out=hv_grouped[:], in_=hv_t[:].rearrange("p t (b n) -> p n b t", n=VARS))
-        hv_codes = keep.tile([P, VARS, BATCH], U32, align_bytes=64)
-        hv_scales = keep.tile([P, VARS, BATCH], U8, align_bytes=64)
-        nc.vector.quantize_mx(
-            out=hv_codes[:].rearrange("p n b -> p (n b)").bitcast(FP8X4),
-            scales=hv_scales[:].rearrange("p n b -> p (n b)"),
-            in_=hv_grouped[:].rearrange("p n b t -> p (n b t)"),
-        )
 
         vec_t = short_ps.tile([P, CHUNKS, P], BF16, tag="short")
         for c in range(CHUNKS):
@@ -134,31 +133,40 @@ def tile_variableselectionnetwork_pb_s_kernel(
             out=vecs[:], in_=vec_t[:, :, : len(vectors) * VARS].rearrange("p c r -> p r c")
         )
 
-        def per_feature(vector, n):
-            return vecs[:, VARS * vector + n, :]
+        def per_feature(place, n):
+            return vecs[:, VARS * place + n, :]
 
-        def along_batch(vector, n):
-            return per_feature(vector, n).unsqueeze(2).to_broadcast([P, CHUNKS, BATCH])
+        def along_batch(place, n):
+            return per_feature(place, n).unsqueeze(2).to_broadcast([P, CHUNKS, BATCH])
+
+        hv_codes = keep.tile([P, VARS, BATCH], U32, align_bytes=64)
+        hv_scales = keep.tile([P, VARS, BATCH], U8, align_bytes=64)
+        nc.vector.quantize_mx(
+            out=hv_codes[:].rearrange("p n b -> p (n b)").bitcast(FP8X4),
+            scales=hv_scales[:].rearrange("p n b -> p (n b)"),
+            in_=hv_grouped[:].rearrange("p n b t -> p (n b t)"),
+        )
 
         sel_t = short_ps.tile([P, CHUNKS, P], BF16, tag="short")
         for c in range(CHUNKS):
             nc.tensor.transpose(sel_t[:, c, :], sel_sb[:, c * P : (c + 1) * P], ident_bf[:])
         sel_by_var = sel_t[:].rearrange("p c (b n) -> p n c b", n=VARS)
         gain_rows = keep_ps.tile([P, VARS, PAIRS, P], F32)
-        shifted = []
         for n in range(VARS):
             sel_gain = keep.tile([P, CHUNKS, BATCH], F32, name="sel_gain_%d" % n)
             nc.vector.tensor_tensor(
                 out=sel_gain[:], in0=sel_by_var[:, n], in1=along_batch(GAIN, n), op=ALU.mult
             )
             to_rows(nc, gain_rows[:, n], sel_gain, ident_f)
-            sel_shift = keep.tile([P, CHUNKS, BATCH], F32, name="sel_shift_%d" % n)
+        sel_shift = keep.tile([P, VARS, CHUNKS, BATCH], F32)
+        for n in range(VARS):
             nc.vector.tensor_tensor(
-                out=sel_shift[:], in0=sel_by_var[:, n], in1=along_batch(SHIFT, n), op=ALU.mult
+                out=sel_shift[:, n], in0=sel_by_var[:, n], in1=along_batch(SHIFT, n), op=ALU.mult
             )
-            shifted.append(sel_shift)
         shift_sum = keep.tile([P, CHUNKS, BATCH], F32)
-        nc.vector.tensor_tensor(out=shift_sum[:], in0=shifted[0][:], in1=shifted[1][:], op=ALU.add)
+        nc.vector.tensor_tensor(
+            out=shift_sum[:], in0=sel_shift[:, 0], in1=sel_shift[:, 1], op=ALU.add
+        )
         shift_rows = keep_ps.tile([P, PAIRS, P], F32)
         to_rows(nc, shift_rows, shift_sum, ident_f)
 
@@ -172,10 +180,13 @@ def tile_variableselectionnetwork_pb_s_kernel(
 
         e1_codes = keep.tile([P, VARS, BATCH], U32, align_bytes=64)
         e1_scales = keep.tile([P, VARS, BATCH], U8, align_bytes=64)
-        for n in range(VARS):
-            w1 = quantise_weight(nc, keep, raw1[n], "w1_%d" % n)
-            e1_acc = acc_ps.tile([P, CHUNKS, BATCH], F32, tag="acc")
-            weight_times_batch(nc, e1_acc, w1, (hv_codes[:, n, :], hv_scales[:, n, :]))
+
+        def product(weight, codes, scales, n):
+            acc = acc_ps.tile([P, CHUNKS, BATCH], F32, name="acc", tag="acc")
+            multiply(nc, acc, weight, codes[:, n, :], scales[:, n, :])
+            return acc
+
+        def quantise_e1(e1_acc, n):
             e1_grouped = keep.tile([P, BATCH, PACK], BF16, name="e1_grouped_%d" % n, align_bytes=64)
             nc.vector.tensor_tensor(
                 out=e1_grouped[:],
@@ -189,11 +200,7 @@ def tile_variableselectionnetwork_pb_s_kernel(
                 in_=e1_grouped[:].rearrange("p b c -> p (b c)"),
             )
 
-        gates = []
-        for n in range(VARS):
-            w4 = quantise_weight(nc, keep, raw4[n], "w4_%d" % n)
-            gate_acc = acc_ps.tile([P, CHUNKS, BATCH], F32, tag="acc")
-            weight_times_batch(nc, gate_acc, w4, (e1_codes[:, n, :], e1_scales[:, n, :]))
+        def sigmoid(gate_acc, n):
             gate = keep.tile([P, CHUNKS, BATCH], F32, name="gate_%d" % n)
             for c in range(CHUNKS):
                 nc.scalar.activation(
@@ -202,69 +209,115 @@ def tile_variableselectionnetwork_pb_s_kernel(
                     func=ACT.Sigmoid,
                     bias=per_feature(VB4, n)[:, c : c + 1],
                 )
-            gates.append(gate)
+            return gate
 
-        total = shift_rows[:].rearrange("p j q -> p (j q)")
-        for n in range(VARS):
-            w5 = quantise_weight(nc, keep, raw5[n], "w5_%d" % n)
-            value_acc = acc_ps.tile([P, CHUNKS, BATCH], F32, tag="acc")
-            weight_times_batch(nc, value_acc, w5, (e1_codes[:, n, :], e1_scales[:, n, :]))
+        def gated_value_rows(value_acc, gate, n):
             gv = keep.tile([P, CHUNKS, BATCH], F32, name="gv_%d" % n)
             for c in range(CHUNKS):
                 nc.vector.scalar_tensor_tensor(
                     out=gv[:, c, :],
                     in0=value_acc[:, c, :],
                     scalar=per_feature(VB5, n)[:, c : c + 1],
-                    in1=gates[n][:, c, :],
+                    in1=gate[:, c, :],
                     op0=ALU.add,
                     op1=ALU.mult,
                 )
-            gv_rows = rows_ps.tile([P, PAIRS, P], F32, tag="rows")
+            gv_rows = rows_ps.tile([P, PAIRS, P], F32, name="gv_rows", tag="rows")
             to_rows(nc, gv_rows, gv, ident_f)
-            resid = keep.tile([P, PAIRS * P], F32, name="resid_%d" % n)
+            return gv_rows
+
+        resid = keep.tile([P, VARS, PAIRS * P], F32)
+        own = keep.tile([P, VARS, 2], F32)
+
+        def residual_stats(gv_rows, n):
             nc.vector.tensor_tensor(
-                out=resid[:],
+                out=resid[:, n, :],
                 in0=gv_rows[:].rearrange("p j q -> p (j q)"),
                 in1=x_rows[:, n].rearrange("p j q -> p (j q)"),
                 op=ALU.add,
             )
-
             stats = keep.tile([P, 6], F32, name="stats_%d" % n)
-            nc.vector.bn_stats(out=stats[:], in_=resid[:])
-            own = keep.tile([P, 2], F32, name="own_%d" % n)
-            nc.vector.bn_aggr(out=own[:], in_=stats[:])
-            sums = short_ps.tile([P, 2], F32, tag="short")
-            nc.tensor.matmul(
-                out=sums[:], lhsT=pair[:].rearrange("p h b -> p (h b)"), rhs=own[:], start=True, stop=True
-            )
-            avg = keep.tile([P, 2], F32, name="avg_%d" % n)
-            nc.vector.tensor_scalar(
-                out=avg[:], in0=sums[:], scalar1=1.0 / HALVES, scalar2=None, op0=ALU.mult
-            )
-            mean = avg[:, 0:1]
-            dev = keep.tile([P, 1], F32, name="dev_%d" % n)
-            nc.vector.tensor_tensor(out=dev[:], in0=own[:, 0:1], in1=mean, op=ALU.subtract)
-            dev_sq = keep.tile([P, 1], F32, name="dev_sq_%d" % n)
-            nc.vector.tensor_scalar(
-                out=dev_sq[:], in0=dev[:], scalar1=dev[:], scalar2=EPS, op0=ALU.mult, op1=ALU.add
-            )
-            var_eps = keep.tile([P, 1], F32, name="var_eps_%d" % n)
-            nc.vector.tensor_tensor(out=var_eps[:], in0=dev_sq[:], in1=avg[:, 1:2], op=ALU.add)
-            rstd = keep.tile([P, 1], F32, name="rstd_%d" % n)
-            nc.gpsimd.tensor_tensor(out=rstd[:], in0=var_eps[:], in1=minus_half[:], op=ALU.pow)
+            nc.vector.bn_stats(out=stats[:], in_=resid[:, n, :])
+            nc.vector.bn_aggr(out=own[:, n, :], in_=stats[:])
 
-            weighted = keep.tile([P, PAIRS * P], F32, name="weighted_%d" % n)
+        g_w1_0 = regroup(nc, keep, raw1[0], "w1_0")
+
+        g_w1_1 = regroup(nc, keep, raw1[1], "w1_1")
+        w1_0 = quantise(nc, keep, g_w1_0, "w1_0")
+        e1_acc_0 = product(w1_0, hv_codes, hv_scales, 0)
+
+        g_w4_0 = regroup(nc, keep, raw4[0], "w4_0")
+        w1_1 = quantise(nc, keep, g_w1_1, "w1_1")
+        e1_acc_1 = product(w1_1, hv_codes, hv_scales, 1)
+        quantise_e1(e1_acc_0, 0)
+
+        g_w4_1 = regroup(nc, keep, raw4[1], "w4_1")
+        w4_0 = quantise(nc, keep, g_w4_0, "w4_0")
+        gate_acc_0 = product(w4_0, e1_codes, e1_scales, 0)
+        quantise_e1(e1_acc_1, 1)
+
+        g_w5_0 = regroup(nc, keep, raw5[0], "w5_0")
+        w4_1 = quantise(nc, keep, g_w4_1, "w4_1")
+        gate_acc_1 = product(w4_1, e1_codes, e1_scales, 1)
+        gate_0 = sigmoid(gate_acc_0, 0)
+
+        g_w5_1 = regroup(nc, keep, raw5[1], "w5_1")
+        w5_0 = quantise(nc, keep, g_w5_0, "w5_0")
+        value_acc_0 = product(w5_0, e1_codes, e1_scales, 0)
+        gate_1 = sigmoid(gate_acc_1, 1)
+        nc.scalar.activation(out=warm[:, 1:2], in_=one[:], func=ACT.Sqrt)
+
+        w5_1 = quantise(nc, keep, g_w5_1, "w5_1")
+        value_acc_1 = product(w5_1, e1_codes, e1_scales, 1)
+        gv_rows_0 = gated_value_rows(value_acc_0, gate_0, 0)
+
+        gv_rows_1 = gated_value_rows(value_acc_1, gate_1, 1)
+        residual_stats(gv_rows_0, 0)
+        residual_stats(gv_rows_1, 1)
+
+        sums = short_ps.tile([P, VARS, 2], F32, tag="short")
+        nc.tensor.matmul(
+            out=sums[:].rearrange("p n s -> p (n s)"),
+            lhsT=pair[:].rearrange("p h b -> p (h b)"),
+            rhs=own[:].rearrange("p n s -> p (n s)"),
+            start=True,
+            stop=True,
+        )
+        avg = keep.tile([P, VARS, 2], F32)
+        nc.vector.tensor_scalar(
+            out=avg[:], in0=sums[:], scalar1=1.0 / HALVES, scalar2=None, op0=ALU.mult
+        )
+        dev = keep.tile([P, VARS], F32)
+        nc.vector.tensor_tensor(out=dev[:], in0=own[:, :, 0], in1=avg[:, :, 0], op=ALU.subtract)
+        dev_sq = keep.tile([P, VARS], F32)
+        nc.vector.tensor_tensor(out=dev_sq[:], in0=dev[:], in1=dev[:], op=ALU.mult)
+        var = keep.tile([P, VARS], F32)
+        nc.vector.tensor_tensor(out=var[:], in0=dev_sq[:], in1=avg[:, :, 1], op=ALU.add)
+        std = keep.tile([P, VARS], F32)
+        nc.scalar.activation(out=std[:], in_=var[:], func=ACT.Sqrt, bias=EPS)
+
+        weighted = keep.tile([P, VARS, PAIRS * P], F32)
+        for n in range(VARS):
             nc.vector.scalar_tensor_tensor(
-                out=weighted[:],
-                in0=resid[:],
-                scalar=mean,
+                out=weighted[:, n, :],
+                in0=resid[:, n, :],
+                scalar=avg[:, n, 0:1],
                 in1=gain_rows[:, n].rearrange("p j q -> p (j q)"),
                 op0=ALU.subtract,
                 op1=ALU.mult,
             )
+        rstd = keep.tile([P, VARS], F32)
+        nc.vector.reciprocal(out=rstd[:], in_=std[:])
+        total = shift_rows[:].rearrange("p j q -> p (j q)")
+        for n in range(VARS):
             summed = keep.tile([P, PAIRS * P], F32, name="summed_%d" % n)
             nc.vector.scalar_tensor_tensor(
-                out=summed[:], in0=weighted[:], scalar=rstd[:], in1=total, op0=ALU.mult, op1=ALU.add
+                out=summed[:],
+                in0=weighted[:, n, :],
+                scalar=rstd[:, n : n + 1],
+                in1=total,
+                op0=ALU.mult,
+                op1=ALU.add,
             )
             total = summed[:]
 

@@ -22,7 +22,7 @@ PAIRS = CHUNKS // HALVES
 EPS = 1e-5
 FLOPS = 2 * 3 * VARS * BATCH * FEAT * FEAT
 
-SCALAR_COLS = 256
+SCALAR_COLS = 320
 RUN = 4
 VB1 = 0
 VB4 = 1
@@ -85,7 +85,7 @@ def tile_variableselectionnetwork_pb_s_kernel(
     nc = tc.nc
     with ExitStack() as stack:
         keep = stack.enter_context(tc.tile_pool(name="keep", bufs=1))
-        short_ps = stack.enter_context(tc.psum_pool(name="short_ps", bufs=2))
+        short_ps = stack.enter_context(tc.psum_pool(name="short_ps", bufs=1))
         acc_ps = stack.enter_context(tc.psum_pool(name="acc_ps", bufs=2))
         rows_ps = stack.enter_context(tc.psum_pool(name="rows_ps", bufs=2))
         keep_ps = stack.enter_context(tc.psum_pool(name="keep_ps", bufs=1))
@@ -99,10 +99,6 @@ def tile_variableselectionnetwork_pb_s_kernel(
         ident_f = keep.tile([P, P], F32)
         nc.vector.memset(ident_f[:], 0.0)
         make_identity(nc, ident_f[:], nomemset=True)
-        one = keep.tile([P, 1], F32)
-        nc.vector.memset(one[:], 1.0)
-        warm = keep.tile([P, 2], F32)
-        nc.scalar.activation(out=warm[:, 0:1], in_=one[:], func=ACT.Sigmoid)
 
         hv_sb = keep.tile([P, FEAT], BF16)
         nc.sync.dma_start(out=hv_sb[:], in_=hv.rearrange("b n k -> (b n) k"))
@@ -119,19 +115,39 @@ def tile_variableselectionnetwork_pb_s_kernel(
         for h in range(HALVES):
             nc.gpsimd.dma_start(out=x_rows[h * BATCH : (h + 1) * BATCH], in_=x_halves[h])
 
+        one = keep.tile([P, 1], F32)
+        nc.vector.memset(one[:], 1.0)
+        warm = keep.tile([P, 2], F32)
+        nc.scalar.activation(out=warm[:, 0:1], in_=one[:], func=ACT.Sigmoid)
+
         hv_t = short_ps.tile([P, PACK, P], BF16, tag="short")
         for t in range(PACK):
             nc.tensor.transpose(hv_t[:, t, :], hv_sb[:, t * P : (t + 1) * P], ident_bf[:])
         hv_grouped = keep.tile([P, VARS, BATCH, PACK], BF16, align_bytes=64)
         nc.scalar.copy(out=hv_grouped[:], in_=hv_t[:].rearrange("p t (b n) -> p n b t", n=VARS))
 
+        hv_codes = keep.tile([P, VARS, BATCH], U32, align_bytes=64)
+        hv_scales = keep.tile([P, VARS, BATCH], U8, align_bytes=64)
+
+        def quantise_hv():
+            nc.vector.quantize_mx(
+                out=hv_codes[:].rearrange("p n b -> p (n b)").bitcast(FP8X4),
+                scales=hv_scales[:].rearrange("p n b -> p (n b)"),
+                in_=hv_grouped[:].rearrange("p n b t -> p (n b t)"),
+            )
+
+        sel_t = keep_ps.tile([P, CHUNKS, P], BF16)
+        for c in range(CHUNKS):
+            nc.tensor.transpose(sel_t[:, c, :], sel_sb[:, c * P : (c + 1) * P], ident_bf[:])
         vec_t = short_ps.tile([P, CHUNKS, P], BF16, tag="short")
         for c in range(CHUNKS):
             nc.tensor.transpose(vec_t[:, c, :], vec_rows[:, c * P : (c + 1) * P], ident_bf[:])
         vecs = keep.tile([P, len(vectors) * VARS, CHUNKS], F32)
-        nc.vector.tensor_copy(
-            out=vecs[:], in_=vec_t[:, :, : len(vectors) * VARS].rearrange("p c r -> p r c")
-        )
+
+        def copy_vectors():
+            nc.vector.tensor_copy(
+                out=vecs[:], in_=vec_t[:, :, : len(vectors) * VARS].rearrange("p c r -> p r c")
+            )
 
         def per_feature(place, n):
             return vecs[:, VARS * place + n, :]
@@ -139,44 +155,32 @@ def tile_variableselectionnetwork_pb_s_kernel(
         def along_batch(place, n):
             return per_feature(place, n).unsqueeze(2).to_broadcast([P, CHUNKS, BATCH])
 
-        hv_codes = keep.tile([P, VARS, BATCH], U32, align_bytes=64)
-        hv_scales = keep.tile([P, VARS, BATCH], U8, align_bytes=64)
-        nc.vector.quantize_mx(
-            out=hv_codes[:].rearrange("p n b -> p (n b)").bitcast(FP8X4),
-            scales=hv_scales[:].rearrange("p n b -> p (n b)"),
-            in_=hv_grouped[:].rearrange("p n b t -> p (n b t)"),
-        )
-
-        sel_t = short_ps.tile([P, CHUNKS, P], BF16, tag="short")
-        for c in range(CHUNKS):
-            nc.tensor.transpose(sel_t[:, c, :], sel_sb[:, c * P : (c + 1) * P], ident_bf[:])
         sel_by_var = sel_t[:].rearrange("p c (b n) -> p n c b", n=VARS)
         gain_rows = keep_ps.tile([P, VARS, PAIRS, P], F32)
-        for n in range(VARS):
-            sel_gain = keep.tile([P, CHUNKS, BATCH], F32, name="sel_gain_%d" % n)
-            nc.vector.tensor_tensor(
-                out=sel_gain[:], in0=sel_by_var[:, n], in1=along_batch(GAIN, n), op=ALU.mult
-            )
-            to_rows(nc, gain_rows[:, n], sel_gain, ident_f)
-        sel_shift = keep.tile([P, VARS, CHUNKS, BATCH], F32)
-        for n in range(VARS):
-            nc.vector.tensor_tensor(
-                out=sel_shift[:, n], in0=sel_by_var[:, n], in1=along_batch(SHIFT, n), op=ALU.mult
-            )
-        shift_sum = keep.tile([P, CHUNKS, BATCH], F32)
-        nc.vector.tensor_tensor(
-            out=shift_sum[:], in0=sel_shift[:, 0], in1=sel_shift[:, 1], op=ALU.add
-        )
         shift_rows = keep_ps.tile([P, PAIRS, P], F32)
-        to_rows(nc, shift_rows, shift_sum, ident_f)
 
-        pair = keep.tile([P, HALVES, BATCH], F32)
-        nc.vector.tensor_tensor(
-            out=pair[:],
-            in0=ident_f[:, :BATCH].unsqueeze(1).to_broadcast([P, HALVES, BATCH]),
-            in1=ident_f[:, BATCH:].unsqueeze(1).to_broadcast([P, HALVES, BATCH]),
-            op=ALU.add,
-        )
+        def selection_times_gain():
+            for n in range(VARS):
+                sel_gain = keep.tile([P, CHUNKS, BATCH], F32, name="sel_gain_%d" % n)
+                nc.vector.tensor_tensor(
+                    out=sel_gain[:], in0=sel_by_var[:, n], in1=along_batch(GAIN, n), op=ALU.mult
+                )
+                to_rows(nc, gain_rows[:, n], sel_gain, ident_f)
+
+        sel_shift = keep.tile([P, VARS, CHUNKS, BATCH], F32)
+
+        def selection_times_shift():
+            for n in range(VARS):
+                nc.vector.tensor_tensor(
+                    out=sel_shift[:, n], in0=sel_by_var[:, n], in1=along_batch(SHIFT, n), op=ALU.mult
+                )
+
+        def sum_of_shifts():
+            shift_sum = keep.tile([P, CHUNKS, BATCH], F32)
+            nc.vector.tensor_tensor(
+                out=shift_sum[:], in0=sel_shift[:, 0], in1=sel_shift[:, 1], op=ALU.add
+            )
+            to_rows(nc, shift_rows, shift_sum, ident_f)
 
         e1_codes = keep.tile([P, VARS, BATCH], U32, align_bytes=64)
         e1_scales = keep.tile([P, VARS, BATCH], U8, align_bytes=64)
@@ -241,10 +245,12 @@ def tile_variableselectionnetwork_pb_s_kernel(
             nc.vector.bn_aggr(out=own[:, n, :], in_=stats[:])
 
         g_w1_0 = regroup(nc, keep, raw1[0], "w1_0")
+        quantise_hv()
 
         g_w1_1 = regroup(nc, keep, raw1[1], "w1_1")
         w1_0 = quantise(nc, keep, g_w1_0, "w1_0")
         e1_acc_0 = product(w1_0, hv_codes, hv_scales, 0)
+        copy_vectors()
 
         g_w4_0 = regroup(nc, keep, raw4[0], "w4_0")
         w1_1 = quantise(nc, keep, g_w1_1, "w1_1")
@@ -260,6 +266,13 @@ def tile_variableselectionnetwork_pb_s_kernel(
         w4_1 = quantise(nc, keep, g_w4_1, "w4_1")
         gate_acc_1 = product(w4_1, e1_codes, e1_scales, 1)
         gate_0 = sigmoid(gate_acc_0, 0)
+        pair = keep.tile([P, HALVES, BATCH], F32)
+        nc.vector.tensor_tensor(
+            out=pair[:],
+            in0=ident_f[:, :BATCH].unsqueeze(1).to_broadcast([P, HALVES, BATCH]),
+            in1=ident_f[:, BATCH:].unsqueeze(1).to_broadcast([P, HALVES, BATCH]),
+            op=ALU.add,
+        )
 
         g_w5_1 = regroup(nc, keep, raw5[1], "w5_1")
         w5_0 = quantise(nc, keep, g_w5_0, "w5_0")
@@ -269,8 +282,9 @@ def tile_variableselectionnetwork_pb_s_kernel(
 
         w5_1 = quantise(nc, keep, g_w5_1, "w5_1")
         value_acc_1 = product(w5_1, e1_codes, e1_scales, 1)
-        gv_rows_0 = gated_value_rows(value_acc_0, gate_0, 0)
 
+        gv_rows_0 = gated_value_rows(value_acc_0, gate_0, 0)
+        selection_times_gain()
         gv_rows_1 = gated_value_rows(value_acc_1, gate_1, 1)
         residual_stats(gv_rows_0, 0)
         residual_stats(gv_rows_1, 1)
@@ -283,19 +297,27 @@ def tile_variableselectionnetwork_pb_s_kernel(
             start=True,
             stop=True,
         )
+        selection_times_shift()
         avg = keep.tile([P, VARS, 2], F32)
         nc.vector.tensor_scalar(
             out=avg[:], in0=sums[:], scalar1=1.0 / HALVES, scalar2=None, op0=ALU.mult
         )
         dev = keep.tile([P, VARS], F32)
         nc.vector.tensor_tensor(out=dev[:], in0=own[:, :, 0], in1=avg[:, :, 0], op=ALU.subtract)
-        dev_sq = keep.tile([P, VARS], F32)
-        nc.vector.tensor_tensor(out=dev_sq[:], in0=dev[:], in1=dev[:], op=ALU.mult)
         var = keep.tile([P, VARS], F32)
-        nc.vector.tensor_tensor(out=var[:], in0=dev_sq[:], in1=avg[:, :, 1], op=ALU.add)
+        for n in range(VARS):
+            nc.vector.scalar_tensor_tensor(
+                out=var[:, n : n + 1],
+                in0=dev[:, n : n + 1],
+                scalar=dev[:, n : n + 1],
+                in1=avg[:, n, 1:2],
+                op0=ALU.mult,
+                op1=ALU.add,
+            )
         std = keep.tile([P, VARS], F32)
         nc.scalar.activation(out=std[:], in_=var[:], func=ACT.Sqrt, bias=EPS)
 
+        sum_of_shifts()
         weighted = keep.tile([P, VARS, PAIRS * P], F32)
         for n in range(VARS):
             nc.vector.scalar_tensor_tensor(

@@ -100,15 +100,16 @@ def tile_variableselectionnetwork_pb_s_kernel(
         nc.vector.memset(ident_f[:], 0.0)
         make_identity(nc, ident_f[:], nomemset=True)
 
+        raw1 = [load_weight(nc, keep, vW1[0, :, :], "w1_0")]
         hv_sb = keep.tile([P, FEAT], BF16)
         nc.sync.dma_start(out=hv_sb[:], in_=hv.rearrange("b n k -> (b n) k"))
         vectors = {VB1: vb1, VB4: vb4, VB5: vb5, GAIN: vlng, SHIFT: vlnb}
         for place, vector in vectors.items():
-            nc.scalar.dma_start(out=vec_rows[VARS * place : VARS * (place + 1), :], in_=vector)
+            nc.sync.dma_start(out=vec_rows[VARS * place : VARS * (place + 1), :], in_=vector)
+        raw1.append(load_weight(nc, keep, vW1[1, :, :], "w1_1"))
+        raw4 = [load_weight(nc, keep, vW4[n, :, :], "w4_%d" % n) for n in range(VARS)]
         sel_sb = keep.tile([P, FEAT], BF16)
         nc.sync.dma_start(out=sel_sb[:], in_=sel_w.rearrange("b n f -> (b n) f"))
-        raw1 = [load_weight(nc, keep, vW1[n, :, :], "w1_%d" % n) for n in range(VARS)]
-        raw4 = [load_weight(nc, keep, vW4[n, :, :], "w4_%d" % n) for n in range(VARS)]
         raw5 = [load_weight(nc, keep, vW5[n, :, :], "w5_%d" % n) for n in range(VARS)]
         x_rows = keep.tile([P, VARS, PAIRS, P], BF16)
         x_halves = x.rearrange("b n (j h q) -> h b n j q", h=HALVES, q=P)
@@ -119,6 +120,8 @@ def tile_variableselectionnetwork_pb_s_kernel(
         nc.vector.memset(one[:], 1.0)
         warm = keep.tile([P, 2], F32)
         nc.scalar.activation(out=warm[:, 0:1], in_=one[:], func=ACT.Sigmoid)
+
+        g_w1_0 = regroup(nc, keep, raw1[0], "w1_0")
 
         hv_t = short_ps.tile([P, PACK, P], BF16, tag="short")
         for t in range(PACK):
@@ -137,8 +140,6 @@ def tile_variableselectionnetwork_pb_s_kernel(
             )
 
         sel_t = keep_ps.tile([P, CHUNKS, P], BF16)
-        for c in range(CHUNKS):
-            nc.tensor.transpose(sel_t[:, c, :], sel_sb[:, c * P : (c + 1) * P], ident_bf[:])
         vec_t = short_ps.tile([P, CHUNKS, P], BF16, tag="short")
         for c in range(CHUNKS):
             nc.tensor.transpose(vec_t[:, c, :], vec_rows[:, c * P : (c + 1) * P], ident_bf[:])
@@ -152,30 +153,23 @@ def tile_variableselectionnetwork_pb_s_kernel(
         def per_feature(place, n):
             return vecs[:, VARS * place + n, :]
 
-        def along_batch(place, n):
-            return per_feature(place, n).unsqueeze(2).to_broadcast([P, CHUNKS, BATCH])
+        def both_vars(place):
+            rows = vecs[:, VARS * place : VARS * (place + 1), :]
+            return rows.unsqueeze(3).to_broadcast([P, VARS, CHUNKS, BATCH])
 
         sel_by_var = sel_t[:].rearrange("p c (b n) -> p n c b", n=VARS)
         gain_rows = keep_ps.tile([P, VARS, PAIRS, P], F32)
         shift_rows = keep_ps.tile([P, PAIRS, P], F32)
 
         def selection_times_gain():
+            sel_gain = keep.tile([P, VARS, CHUNKS, BATCH], F32)
+            nc.vector.tensor_tensor(out=sel_gain[:], in0=sel_by_var, in1=both_vars(GAIN), op=ALU.mult)
             for n in range(VARS):
-                sel_gain = keep.tile([P, CHUNKS, BATCH], F32, name="sel_gain_%d" % n)
-                nc.vector.tensor_tensor(
-                    out=sel_gain[:], in0=sel_by_var[:, n], in1=along_batch(GAIN, n), op=ALU.mult
-                )
-                to_rows(nc, gain_rows[:, n], sel_gain, ident_f)
-
-        sel_shift = keep.tile([P, VARS, CHUNKS, BATCH], F32)
+                to_rows(nc, gain_rows[:, n], sel_gain[:, n], ident_f)
 
         def selection_times_shift():
-            for n in range(VARS):
-                nc.vector.tensor_tensor(
-                    out=sel_shift[:, n], in0=sel_by_var[:, n], in1=along_batch(SHIFT, n), op=ALU.mult
-                )
-
-        def sum_of_shifts():
+            sel_shift = keep.tile([P, VARS, CHUNKS, BATCH], F32)
+            nc.vector.tensor_tensor(out=sel_shift[:], in0=sel_by_var, in1=both_vars(SHIFT), op=ALU.mult)
             shift_sum = keep.tile([P, CHUNKS, BATCH], F32)
             nc.vector.tensor_tensor(
                 out=shift_sum[:], in0=sel_shift[:, 0], in1=sel_shift[:, 1], op=ALU.add
@@ -244,10 +238,45 @@ def tile_variableselectionnetwork_pb_s_kernel(
             nc.vector.bn_stats(out=stats[:], in_=resid[:, n, :])
             nc.vector.bn_aggr(out=own[:, n, :], in_=stats[:])
 
-        g_w1_0 = regroup(nc, keep, raw1[0], "w1_0")
-        quantise_hv()
+        def row_statistics(n):
+            row = short_ps.tile([P, 2], F32, name="row", tag="short")
+            nc.tensor.matmul(
+                out=row[:], lhsT=pair[:].rearrange("p h b -> p (h b)"), rhs=own[:, n, :], start=True, stop=True
+            )
+            return row
+
+        def one_over_std(row, n):
+            dev = keep.tile([P, 1], F32, name="dev_%d" % n)
+            nc.vector.tensor_tensor(out=dev[:], in0=own[:, n, 0:1], in1=row[:, 0:1], op=ALU.subtract)
+            var = keep.tile([P, 1], F32, name="var_%d" % n)
+            nc.vector.scalar_tensor_tensor(
+                out=var[:], in0=dev[:], scalar=dev[:], in1=row[:, 1:2], op0=ALU.mult, op1=ALU.add
+            )
+            rstd = keep.tile([P, 1], F32, name="rstd_%d" % n)
+            nc.scalar.activation(out=rstd[:], in_=var[:], func=ACT.Abs_reciprocal_sqrt, bias=EPS)
+            return rstd
+
+        def centred_times_gain(row, n):
+            weighted = keep.tile([P, PAIRS * P], F32, name="weighted_%d" % n)
+            nc.vector.scalar_tensor_tensor(
+                out=weighted[:],
+                in0=resid[:, n, :],
+                scalar=row[:, 0:1],
+                in1=gain_rows[:, n].rearrange("p j q -> p (j q)"),
+                op0=ALU.subtract,
+                op1=ALU.mult,
+            )
+            return weighted
+
+        def scaled_plus(weighted, rstd, addend, n):
+            summed = keep.tile([P, PAIRS * P], F32, name="summed_%d" % n)
+            nc.vector.scalar_tensor_tensor(
+                out=summed[:], in0=weighted[:], scalar=rstd[:], in1=addend, op0=ALU.mult, op1=ALU.add
+            )
+            return summed[:]
 
         g_w1_1 = regroup(nc, keep, raw1[1], "w1_1")
+        quantise_hv()
         w1_0 = quantise(nc, keep, g_w1_0, "w1_0")
         e1_acc_0 = product(w1_0, hv_codes, hv_scales, 0)
         copy_vectors()
@@ -261,89 +290,49 @@ def tile_variableselectionnetwork_pb_s_kernel(
         w4_0 = quantise(nc, keep, g_w4_0, "w4_0")
         gate_acc_0 = product(w4_0, e1_codes, e1_scales, 0)
         quantise_e1(e1_acc_1, 1)
+        half_ident = keep.tile([P, P], F32)
+        nc.scalar.mul(out=half_ident[:], in_=ident_f[:], mul=1.0 / HALVES)
+        for c in range(CHUNKS):
+            nc.tensor.transpose(sel_t[:, c, :], sel_sb[:, c * P : (c + 1) * P], ident_bf[:])
 
         g_w5_0 = regroup(nc, keep, raw5[0], "w5_0")
         w4_1 = quantise(nc, keep, g_w4_1, "w4_1")
         gate_acc_1 = product(w4_1, e1_codes, e1_scales, 1)
         gate_0 = sigmoid(gate_acc_0, 0)
-        pair = keep.tile([P, HALVES, BATCH], F32)
-        nc.vector.tensor_tensor(
-            out=pair[:],
-            in0=ident_f[:, :BATCH].unsqueeze(1).to_broadcast([P, HALVES, BATCH]),
-            in1=ident_f[:, BATCH:].unsqueeze(1).to_broadcast([P, HALVES, BATCH]),
-            op=ALU.add,
-        )
+        selection_times_gain()
 
         g_w5_1 = regroup(nc, keep, raw5[1], "w5_1")
         w5_0 = quantise(nc, keep, g_w5_0, "w5_0")
         value_acc_0 = product(w5_0, e1_codes, e1_scales, 0)
         gate_1 = sigmoid(gate_acc_1, 1)
-        nc.scalar.activation(out=warm[:, 1:2], in_=one[:], func=ACT.Sqrt)
+        nc.scalar.activation(out=warm[:, 1:2], in_=one[:], func=ACT.Abs_reciprocal_sqrt)
+        selection_times_shift()
+        pair = keep.tile([P, HALVES, BATCH], F32)
+        nc.vector.tensor_tensor(
+            out=pair[:],
+            in0=half_ident[:, :BATCH].unsqueeze(1).to_broadcast([P, HALVES, BATCH]),
+            in1=half_ident[:, BATCH:].unsqueeze(1).to_broadcast([P, HALVES, BATCH]),
+            op=ALU.add,
+        )
+
+        gv_rows_0 = gated_value_rows(value_acc_0, gate_0, 0)
 
         w5_1 = quantise(nc, keep, g_w5_1, "w5_1")
         value_acc_1 = product(w5_1, e1_codes, e1_scales, 1)
 
-        gv_rows_0 = gated_value_rows(value_acc_0, gate_0, 0)
-        selection_times_gain()
-        gv_rows_1 = gated_value_rows(value_acc_1, gate_1, 1)
         residual_stats(gv_rows_0, 0)
+        row_0 = row_statistics(0)
+        gv_rows_1 = gated_value_rows(value_acc_1, gate_1, 1)
+        rstd_0 = one_over_std(row_0, 0)
+        weighted_0 = centred_times_gain(row_0, 0)
         residual_stats(gv_rows_1, 1)
-
-        sums = short_ps.tile([P, VARS, 2], F32, tag="short")
-        nc.tensor.matmul(
-            out=sums[:].rearrange("p n s -> p (n s)"),
-            lhsT=pair[:].rearrange("p h b -> p (h b)"),
-            rhs=own[:].rearrange("p n s -> p (n s)"),
-            start=True,
-            stop=True,
-        )
-        selection_times_shift()
-        avg = keep.tile([P, VARS, 2], F32)
-        nc.vector.tensor_scalar(
-            out=avg[:], in0=sums[:], scalar1=1.0 / HALVES, scalar2=None, op0=ALU.mult
-        )
-        dev = keep.tile([P, VARS], F32)
-        nc.vector.tensor_tensor(out=dev[:], in0=own[:, :, 0], in1=avg[:, :, 0], op=ALU.subtract)
-        var = keep.tile([P, VARS], F32)
-        for n in range(VARS):
-            nc.vector.scalar_tensor_tensor(
-                out=var[:, n : n + 1],
-                in0=dev[:, n : n + 1],
-                scalar=dev[:, n : n + 1],
-                in1=avg[:, n, 1:2],
-                op0=ALU.mult,
-                op1=ALU.add,
-            )
-        std = keep.tile([P, VARS], F32)
-        nc.scalar.activation(out=std[:], in_=var[:], func=ACT.Sqrt, bias=EPS)
-
-        sum_of_shifts()
-        weighted = keep.tile([P, VARS, PAIRS * P], F32)
-        for n in range(VARS):
-            nc.vector.scalar_tensor_tensor(
-                out=weighted[:, n, :],
-                in0=resid[:, n, :],
-                scalar=avg[:, n, 0:1],
-                in1=gain_rows[:, n].rearrange("p j q -> p (j q)"),
-                op0=ALU.subtract,
-                op1=ALU.mult,
-            )
-        rstd = keep.tile([P, VARS], F32)
-        nc.vector.reciprocal(out=rstd[:], in_=std[:])
-        total = shift_rows[:].rearrange("p j q -> p (j q)")
-        for n in range(VARS):
-            summed = keep.tile([P, PAIRS * P], F32, name="summed_%d" % n)
-            nc.vector.scalar_tensor_tensor(
-                out=summed[:],
-                in0=weighted[:, n, :],
-                scalar=rstd[:, n : n + 1],
-                in1=total,
-                op0=ALU.mult,
-                op1=ALU.add,
-            )
-            total = summed[:]
+        row_1 = row_statistics(1)
+        total_0 = scaled_plus(weighted_0, rstd_0, shift_rows[:].rearrange("p j q -> p (j q)"), 0)
+        rstd_1 = one_over_std(row_1, 1)
+        weighted_1 = centred_times_gain(row_1, 1)
+        total = scaled_plus(weighted_1, rstd_1, total_0, 1)
 
         out_halves = out.rearrange("b (j h q) -> h b j q", h=HALVES, q=P)
         result = total.rearrange("p (j q) -> p j q", q=P)
         nc.sync.dma_start(out=out_halves[0], in_=result[:BATCH])
-        nc.scalar.dma_start(out=out_halves[1], in_=result[BATCH:])
+        nc.sync.dma_start(out=out_halves[1], in_=result[BATCH:])

@@ -21,62 +21,9 @@ HALVES = P // BATCH
 PAIRS = CHUNKS // HALVES
 EPS = 1e-5
 FLOPS = 2 * 3 * VARS * BATCH * FEAT * FEAT
-
-SCALAR_COLS = 320
 RUN = 4
-VB1 = 0
-VB4 = 1
-VB5 = 2
-GAIN = 3
-SHIFT = 4
-
-
-def load_weight(nc, pool, weight, label):
-    raw = pool.tile([P, PACK, FEAT], BF16, name="raw_%s" % label)
-    nc.sync.dma_start(out=raw[:], in_=weight.rearrange("(t p) c -> p t c", p=P))
-    return raw
-
-
-def regroup(nc, pool, raw, label):
-    grouped = pool.tile([P, FEAT, PACK], BF16, name="grouped_%s" % label, align_bytes=64)
-    source = raw[:].rearrange("p t (c i) -> p c t i", i=RUN)
-    target = grouped[:].rearrange("p (c i) t -> p c t i", i=RUN)
-    split = SCALAR_COLS // RUN
-    nc.scalar.copy(out=target[:, :split], in_=source[:, :split])
-    nc.vector.tensor_copy(out=target[:, split:], in_=source[:, split:])
-    return grouped
-
-
-def quantise(nc, pool, grouped, label):
-    codes = pool.tile([P, FEAT], U32, name="codes_%s" % label, align_bytes=64)
-    scales = pool.tile([P, FEAT], U8, name="scales_%s" % label, align_bytes=64)
-    nc.vector.quantize_mx(
-        out=codes[:].bitcast(FP8X4),
-        scales=scales[:],
-        in_=grouped[:].rearrange("p c t -> p (c t)"),
-    )
-    return codes, scales
-
-
-def multiply(nc, acc, weight, moving_codes, moving_scales):
-    codes, scales = weight
-    for c in range(CHUNKS):
-        cols = slice(c * P, (c + 1) * P)
-        nc.tensor.matmul_mx(
-            out=acc[:, c, :],
-            lhsT=codes[:, cols].bitcast(FP8X4),
-            lhsT_scale=scales[:, cols],
-            rhs=moving_codes.bitcast(FP8X4),
-            rhs_scale=moving_scales,
-            start=True,
-            stop=True,
-        )
-
-
-def to_rows(nc, rows, by_feature, identity):
-    for j in range(PAIRS):
-        chunk_pair = by_feature[:, j * HALVES : (j + 1) * HALVES, :]
-        nc.tensor.transpose(rows[:, j, :], chunk_pair.rearrange("p h b -> p (h b)"), identity[:])
+VB1, VB4, VB5, GAIN, SHIFT = 0, 1, 2, 3, 4
+SHARE = {"w1_0": 256, "w1_1": 288, "w4_0": 288, "w4_1": 288, "w5_0": 288, "w5_1": 288}
 
 
 def tile_variableselectionnetwork_pb_s_kernel(
@@ -87,7 +34,6 @@ def tile_variableselectionnetwork_pb_s_kernel(
         keep = stack.enter_context(tc.tile_pool(name="keep", bufs=1))
         short_ps = stack.enter_context(tc.psum_pool(name="short_ps", bufs=1))
         acc_ps = stack.enter_context(tc.psum_pool(name="acc_ps", bufs=2))
-        rows_ps = stack.enter_context(tc.psum_pool(name="rows_ps", bufs=2))
         keep_ps = stack.enter_context(tc.psum_pool(name="keep_ps", bufs=1))
         stack.enter_context(tc.manual_schedule())
 
@@ -99,151 +45,177 @@ def tile_variableselectionnetwork_pb_s_kernel(
         ident_f = keep.tile([P, P], F32)
         nc.vector.memset(ident_f[:], 0.0)
         make_identity(nc, ident_f[:], nomemset=True)
+        pair = keep.tile([P, P], F32)
+        nc.vector.memset(pair[:], 0.0)
+        for base in (0, BATCH, -BATCH):
+            nc.gpsimd.affine_select(
+                out=pair[:], in_=pair[:], compare_op=ALU.not_equal, fill=1.0 / HALVES, base=base,
+                pattern=[[-1, P]], channel_multiplier=1,
+            )
 
-        raw1 = [load_weight(nc, keep, vW1[0, :, :], "w1_0")]
         hv_sb = keep.tile([P, FEAT], BF16)
         nc.sync.dma_start(out=hv_sb[:], in_=hv.rearrange("b n k -> (b n) k"))
+
+        def load_weight(weight, label, pieces=1):
+            raw = keep.tile([P, PACK, FEAT], BF16, name="raw_%s" % label)
+            view = weight.rearrange("(t p) c -> p t c", p=P)
+            width = FEAT // pieces
+            for i in range(pieces):
+                cols = slice(i * width, (i + 1) * width)
+                nc.sync.dma_start(out=raw[:, :, cols], in_=view[:, :, cols])
+            return raw
+
+        raw = {"w1_0": load_weight(vW1[0, :, :], "w1_0", 2)}
         vectors = {VB1: vb1, VB4: vb4, VB5: vb5, GAIN: vlng, SHIFT: vlnb}
         for place, vector in vectors.items():
             nc.sync.dma_start(out=vec_rows[VARS * place : VARS * (place + 1), :], in_=vector)
-        raw1.append(load_weight(nc, keep, vW1[1, :, :], "w1_1"))
-        raw4 = [load_weight(nc, keep, vW4[n, :, :], "w4_%d" % n) for n in range(VARS)]
-        sel_sb = keep.tile([P, FEAT], BF16)
-        nc.sync.dma_start(out=sel_sb[:], in_=sel_w.rearrange("b n f -> (b n) f"))
-        raw5 = [load_weight(nc, keep, vW5[n, :, :], "w5_%d" % n) for n in range(VARS)]
+        raw["w1_1"] = load_weight(vW1[1, :, :], "w1_1")
+        raw["w4_0"] = load_weight(vW4[0, :, :], "w4_0")
+        raw["w4_1"] = load_weight(vW4[1, :, :], "w4_1")
+        raw["w5_0"] = load_weight(vW5[0, :, :], "w5_0")
+        raw["w5_1"] = load_weight(vW5[1, :, :], "w5_1")
         x_rows = keep.tile([P, VARS, PAIRS, P], BF16)
         x_halves = x.rearrange("b n (j h q) -> h b n j q", h=HALVES, q=P)
         for h in range(HALVES):
-            nc.gpsimd.dma_start(out=x_rows[h * BATCH : (h + 1) * BATCH], in_=x_halves[h])
+            nc.sync.dma_start(out=x_rows[h * BATCH : (h + 1) * BATCH], in_=x_halves[h])
+        sel_sb = keep.tile([P, FEAT], BF16)
+        nc.sync.dma_start(out=sel_sb[:], in_=sel_w.rearrange("b n f -> (b n) f"))
 
         one = keep.tile([P, 1], F32)
         nc.vector.memset(one[:], 1.0)
         warm = keep.tile([P, 2], F32)
         nc.scalar.activation(out=warm[:, 0:1], in_=one[:], func=ACT.Sigmoid)
 
-        g_w1_0 = regroup(nc, keep, raw1[0], "w1_0")
+        grouped = {}
+
+        def regroup(label):
+            g = keep.tile([P, FEAT, PACK], BF16, name="grouped_%s" % label, align_bytes=64)
+            source = raw[label][:].rearrange("p t (c i) -> p c t i", i=RUN)
+            target = g[:].rearrange("p (c i) t -> p c t i", i=RUN)
+            split = SHARE[label] // RUN
+            nc.scalar.copy(out=target[:, :split], in_=source[:, :split])
+            nc.vector.tensor_copy(out=target[:, split:], in_=source[:, split:])
+            grouped[label] = g
+
+        quantised = {}
+
+        def quantise(label):
+            codes = keep.tile([P, FEAT], U32, name="codes_%s" % label, align_bytes=64)
+            scales = keep.tile([P, FEAT], U8, name="scales_%s" % label, align_bytes=64)
+            nc.vector.quantize_mx(
+                out=codes[:].bitcast(FP8X4), scales=scales[:],
+                in_=grouped[label][:].rearrange("p c t -> p (c t)"),
+            )
+            quantised[label] = (codes, scales)
+
+        def product(label, codes, scales, n):
+            acc = acc_ps.tile([P, CHUNKS, BATCH], F32, name="acc", tag="acc")
+            w_codes, w_scales = quantised[label]
+            for c in range(CHUNKS):
+                cols = slice(c * P, (c + 1) * P)
+                nc.tensor.matmul_mx(
+                    out=acc[:, c, :], lhsT=w_codes[:, cols].bitcast(FP8X4), lhsT_scale=w_scales[:, cols],
+                    rhs=codes[:, n, :].bitcast(FP8X4), rhs_scale=scales[:, n, :], start=True, stop=True,
+                )
+            return acc
 
         hv_t = short_ps.tile([P, PACK, P], BF16, tag="short")
         for t in range(PACK):
             nc.tensor.transpose(hv_t[:, t, :], hv_sb[:, t * P : (t + 1) * P], ident_bf[:])
         hv_grouped = keep.tile([P, VARS, BATCH, PACK], BF16, align_bytes=64)
         nc.scalar.copy(out=hv_grouped[:], in_=hv_t[:].rearrange("p t (b n) -> p n b t", n=VARS))
-
         hv_codes = keep.tile([P, VARS, BATCH], U32, align_bytes=64)
         hv_scales = keep.tile([P, VARS, BATCH], U8, align_bytes=64)
 
-        def quantise_hv():
-            nc.vector.quantize_mx(
-                out=hv_codes[:].rearrange("p n b -> p (n b)").bitcast(FP8X4),
-                scales=hv_scales[:].rearrange("p n b -> p (n b)"),
-                in_=hv_grouped[:].rearrange("p n b t -> p (n b t)"),
-            )
+        regroup("w1_0")
+        nc.vector.quantize_mx(
+            out=hv_codes[:].rearrange("p n b -> p (n b)").bitcast(FP8X4),
+            scales=hv_scales[:].rearrange("p n b -> p (n b)"),
+            in_=hv_grouped[:].rearrange("p n b t -> p (n b t)"),
+        )
 
-        sel_t = keep_ps.tile([P, CHUNKS, P], BF16)
         vec_t = short_ps.tile([P, CHUNKS, P], BF16, tag="short")
         for c in range(CHUNKS):
             nc.tensor.transpose(vec_t[:, c, :], vec_rows[:, c * P : (c + 1) * P], ident_bf[:])
         vecs = keep.tile([P, len(vectors) * VARS, CHUNKS], F32)
 
-        def copy_vectors():
-            nc.vector.tensor_copy(
-                out=vecs[:], in_=vec_t[:, :, : len(vectors) * VARS].rearrange("p c r -> p r c")
-            )
-
         def per_feature(place, n):
             return vecs[:, VARS * place + n, :]
 
-        def both_vars(place):
-            rows = vecs[:, VARS * place : VARS * (place + 1), :]
-            return rows.unsqueeze(3).to_broadcast([P, VARS, CHUNKS, BATCH])
-
-        sel_by_var = sel_t[:].rearrange("p c (b n) -> p n c b", n=VARS)
-        gain_rows = keep_ps.tile([P, VARS, PAIRS, P], F32)
-        shift_rows = keep_ps.tile([P, PAIRS, P], F32)
-
-        def selection_times_gain():
-            sel_gain = keep.tile([P, VARS, CHUNKS, BATCH], F32)
-            nc.vector.tensor_tensor(out=sel_gain[:], in0=sel_by_var, in1=both_vars(GAIN), op=ALU.mult)
-            for n in range(VARS):
-                to_rows(nc, gain_rows[:, n], sel_gain[:, n], ident_f)
-
-        def selection_times_shift():
-            sel_shift = keep.tile([P, VARS, CHUNKS, BATCH], F32)
-            nc.vector.tensor_tensor(out=sel_shift[:], in0=sel_by_var, in1=both_vars(SHIFT), op=ALU.mult)
-            shift_sum = keep.tile([P, CHUNKS, BATCH], F32)
-            nc.vector.tensor_tensor(
-                out=shift_sum[:], in0=sel_shift[:, 0], in1=sel_shift[:, 1], op=ALU.add
-            )
-            to_rows(nc, shift_rows, shift_sum, ident_f)
-
         e1_codes = keep.tile([P, VARS, BATCH], U32, align_bytes=64)
         e1_scales = keep.tile([P, VARS, BATCH], U8, align_bytes=64)
+        e1_grouped = {}
 
-        def product(weight, codes, scales, n):
-            acc = acc_ps.tile([P, CHUNKS, BATCH], F32, name="acc", tag="acc")
-            multiply(nc, acc, weight, codes[:, n, :], scales[:, n, :])
-            return acc
-
-        def quantise_e1(e1_acc, n):
-            e1_grouped = keep.tile([P, BATCH, PACK], BF16, name="e1_grouped_%d" % n, align_bytes=64)
+        def e1_add(e1_acc, n):
+            g = keep.tile([P, BATCH, PACK], BF16, name="e1_grouped_%d" % n, align_bytes=64)
             nc.vector.tensor_tensor(
-                out=e1_grouped[:],
-                in0=e1_acc[:].rearrange("p c b -> p b c"),
-                in1=per_feature(VB1, n).unsqueeze(1).to_broadcast([P, BATCH, PACK]),
-                op=ALU.add,
+                out=g[:], in0=e1_acc[:].rearrange("p c b -> p b c"),
+                in1=per_feature(VB1, n).unsqueeze(1).to_broadcast([P, BATCH, PACK]), op=ALU.add,
             )
+            e1_grouped[n] = g
+
+        def e1_quantise(n):
             nc.vector.quantize_mx(
-                out=e1_codes[:, n, :].bitcast(FP8X4),
-                scales=e1_scales[:, n, :],
-                in_=e1_grouped[:].rearrange("p b c -> p (b c)"),
+                out=e1_codes[:, n, :].bitcast(FP8X4), scales=e1_scales[:, n, :],
+                in_=e1_grouped[n][:].rearrange("p b c -> p (b c)"),
             )
 
         def sigmoid(gate_acc, n):
             gate = keep.tile([P, CHUNKS, BATCH], F32, name="gate_%d" % n)
             for c in range(CHUNKS):
                 nc.scalar.activation(
-                    out=gate[:, c, :],
-                    in_=gate_acc[:, c, :],
-                    func=ACT.Sigmoid,
+                    out=gate[:, c, :], in_=gate_acc[:, c, :], func=ACT.Sigmoid,
                     bias=per_feature(VB4, n)[:, c : c + 1],
                 )
             return gate
 
-        def gated_value_rows(value_acc, gate, n):
+        r_ps = [keep_ps.tile([P, PAIRS, P], F32, name="r_ps_%d" % n) for n in range(VARS)]
+
+        def x_into_rows(n):
+            nc.tensor.matmul(
+                out=r_ps[n][:].rearrange("p j q -> p (j q)"), lhsT=ident_bf[:],
+                rhs=x_rows[:, n].rearrange("p j q -> p (j q)"), start=True, stop=False,
+            )
+
+        def add_rows(rows, by_feature, last):
+            for j in range(PAIRS):
+                nc.tensor.matmul(
+                    out=rows[:, j, :],
+                    lhsT=by_feature[:, j * HALVES : (j + 1) * HALVES, :].rearrange("p h b -> p (h b)"),
+                    rhs=ident_f[:], is_transpose=True, start=False, stop=(last and j == PAIRS - 1),
+                )
+
+        def to_rows(rows, by_feature):
+            for j in range(PAIRS):
+                nc.tensor.transpose(
+                    rows[:, j, :], by_feature[:, j * HALVES : (j + 1) * HALVES, :].rearrange("p h b -> p (h b)"), ident_f[:]
+                )
+
+        def gated_value(value_acc, gate, n):
             gv = keep.tile([P, CHUNKS, BATCH], F32, name="gv_%d" % n)
             for c in range(CHUNKS):
                 nc.vector.scalar_tensor_tensor(
-                    out=gv[:, c, :],
-                    in0=value_acc[:, c, :],
-                    scalar=per_feature(VB5, n)[:, c : c + 1],
-                    in1=gate[:, c, :],
-                    op0=ALU.add,
-                    op1=ALU.mult,
+                    out=gv[:, c, :], in0=value_acc[:, c, :], scalar=per_feature(VB5, n)[:, c : c + 1],
+                    in1=gate[:, c, :], op0=ALU.add, op1=ALU.mult,
                 )
-            gv_rows = rows_ps.tile([P, PAIRS, P], F32, name="gv_rows", tag="rows")
-            to_rows(nc, gv_rows, gv, ident_f)
-            return gv_rows
+            add_rows(r_ps[n], gv, True)
 
-        resid = keep.tile([P, VARS, PAIRS * P], F32)
         own = keep.tile([P, VARS, 2], F32)
+        resid = keep.tile([P, VARS, PAIRS * P], F32)
+        stats = {}
 
-        def residual_stats(gv_rows, n):
-            nc.vector.tensor_tensor(
-                out=resid[:, n, :],
-                in0=gv_rows[:].rearrange("p j q -> p (j q)"),
-                in1=x_rows[:, n].rearrange("p j q -> p (j q)"),
-                op=ALU.add,
-            )
-            stats = keep.tile([P, 6], F32, name="stats_%d" % n)
-            nc.vector.bn_stats(out=stats[:], in_=resid[:, n, :])
-            nc.vector.bn_aggr(out=own[:, n, :], in_=stats[:])
+        def row_stats(n):
+            stats[n] = keep.tile([P, 6], F32, name="stats_%d" % n)
+            nc.vector.bn_stats(out=stats[n][:], in_=r_ps[n][:].rearrange("p j q -> p (j q)"))
 
-        def row_statistics(n):
+        def row_aggr(n):
+            nc.vector.bn_aggr(out=own[:, n, :], in_=stats[n][:])
             row = short_ps.tile([P, 2], F32, name="row", tag="short")
-            nc.tensor.matmul(
-                out=row[:], lhsT=pair[:].rearrange("p h b -> p (h b)"), rhs=own[:, n, :], start=True, stop=True
-            )
+            nc.tensor.matmul(out=row[:], lhsT=pair[:], rhs=own[:, n, :], start=True, stop=True)
             return row
+
+        def resid_copy(n):
+            nc.scalar.copy(out=resid[:, n, :], in_=r_ps[n][:].rearrange("p j q -> p (j q)"))
 
         def one_over_std(row, n):
             dev = keep.tile([P, 1], F32, name="dev_%d" % n)
@@ -256,15 +228,24 @@ def tile_variableselectionnetwork_pb_s_kernel(
             nc.scalar.activation(out=rstd[:], in_=var[:], func=ACT.Abs_reciprocal_sqrt, bias=EPS)
             return rstd
 
+        sel_t = keep_ps.tile([P, CHUNKS, P], BF16)
+        gain_rows = keep_ps.tile([P, VARS, PAIRS, P], F32)
+        shift_rows = keep_ps.tile([P, PAIRS, P], F32)
+        sel_gain = keep.tile([P, VARS, CHUNKS, BATCH], F32)
+        sel_shift = keep.tile([P, VARS, CHUNKS, BATCH], F32)
+
+        def selection_times(target, place, n):
+            for c in range(CHUNKS):
+                nc.scalar.activation(
+                    out=target[:, n, c, :], in_=sel_t[:, c, :].rearrange("p (b n) -> p n b", n=VARS)[:, n, :],
+                    func=ACT.Copy, scale=per_feature(place, n)[:, c : c + 1],
+                )
+
         def centred_times_gain(row, n):
             weighted = keep.tile([P, PAIRS * P], F32, name="weighted_%d" % n)
             nc.vector.scalar_tensor_tensor(
-                out=weighted[:],
-                in0=resid[:, n, :],
-                scalar=row[:, 0:1],
-                in1=gain_rows[:, n].rearrange("p j q -> p (j q)"),
-                op0=ALU.subtract,
-                op1=ALU.mult,
+                out=weighted[:], in0=resid[:, n, :], scalar=row[:, 0:1],
+                in1=gain_rows[:, n].rearrange("p j q -> p (j q)"), op0=ALU.subtract, op1=ALU.mult,
             )
             return weighted
 
@@ -275,58 +256,63 @@ def tile_variableselectionnetwork_pb_s_kernel(
             )
             return summed[:]
 
-        g_w1_1 = regroup(nc, keep, raw1[1], "w1_1")
-        quantise_hv()
-        w1_0 = quantise(nc, keep, g_w1_0, "w1_0")
-        e1_acc_0 = product(w1_0, hv_codes, hv_scales, 0)
-        copy_vectors()
+        regroup("w1_1")
+        quantise("w1_0")
+        e1_acc_0 = product("w1_0", hv_codes, hv_scales, 0)
+        nc.vector.tensor_copy(out=vecs[:], in_=vec_t[:, :, : len(vectors) * VARS].rearrange("p c r -> p r c"))
 
-        g_w4_0 = regroup(nc, keep, raw4[0], "w4_0")
-        w1_1 = quantise(nc, keep, g_w1_1, "w1_1")
-        e1_acc_1 = product(w1_1, hv_codes, hv_scales, 1)
-        quantise_e1(e1_acc_0, 0)
+        regroup("w4_0")
+        quantise("w1_1")
+        e1_acc_1 = product("w1_1", hv_codes, hv_scales, 1)
+        e1_add(e1_acc_0, 0)
 
-        g_w4_1 = regroup(nc, keep, raw4[1], "w4_1")
-        w4_0 = quantise(nc, keep, g_w4_0, "w4_0")
-        gate_acc_0 = product(w4_0, e1_codes, e1_scales, 0)
-        quantise_e1(e1_acc_1, 1)
-        half_ident = keep.tile([P, P], F32)
-        nc.scalar.mul(out=half_ident[:], in_=ident_f[:], mul=1.0 / HALVES)
+        regroup("w4_1")
+        e1_quantise(0)
+        quantise("w4_0")
+        gate_acc_0 = product("w4_0", e1_codes, e1_scales, 0)
+        e1_add(e1_acc_1, 1)
+        for n in range(VARS):
+            x_into_rows(n)
         for c in range(CHUNKS):
             nc.tensor.transpose(sel_t[:, c, :], sel_sb[:, c * P : (c + 1) * P], ident_bf[:])
 
-        g_w5_0 = regroup(nc, keep, raw5[0], "w5_0")
-        w4_1 = quantise(nc, keep, g_w4_1, "w4_1")
-        gate_acc_1 = product(w4_1, e1_codes, e1_scales, 1)
+        regroup("w5_0")
+        e1_quantise(1)
+        quantise("w4_1")
+        gate_acc_1 = product("w4_1", e1_codes, e1_scales, 1)
         gate_0 = sigmoid(gate_acc_0, 0)
-        selection_times_gain()
+        selection_times(sel_gain, GAIN, 0)
+        selection_times(sel_gain, GAIN, 1)
+        to_rows(gain_rows[:, 0], sel_gain[:, 0])
+        to_rows(gain_rows[:, 1], sel_gain[:, 1])
 
-        g_w5_1 = regroup(nc, keep, raw5[1], "w5_1")
-        w5_0 = quantise(nc, keep, g_w5_0, "w5_0")
-        value_acc_0 = product(w5_0, e1_codes, e1_scales, 0)
+        regroup("w5_1")
+        quantise("w5_0")
+        value_acc_0 = product("w5_0", e1_codes, e1_scales, 0)
         gate_1 = sigmoid(gate_acc_1, 1)
+        gated_value(value_acc_0, gate_0, 0)
+        quantise("w5_1")
+        value_acc_1 = product("w5_1", e1_codes, e1_scales, 1)
+
         nc.scalar.activation(out=warm[:, 1:2], in_=one[:], func=ACT.Abs_reciprocal_sqrt)
-        selection_times_shift()
-        pair = keep.tile([P, HALVES, BATCH], F32)
-        nc.vector.tensor_tensor(
-            out=pair[:],
-            in0=half_ident[:, :BATCH].unsqueeze(1).to_broadcast([P, HALVES, BATCH]),
-            in1=half_ident[:, BATCH:].unsqueeze(1).to_broadcast([P, HALVES, BATCH]),
-            op=ALU.add,
-        )
-
-        gv_rows_0 = gated_value_rows(value_acc_0, gate_0, 0)
-
-        w5_1 = quantise(nc, keep, g_w5_1, "w5_1")
-        value_acc_1 = product(w5_1, e1_codes, e1_scales, 1)
-
-        residual_stats(gv_rows_0, 0)
-        row_0 = row_statistics(0)
-        gv_rows_1 = gated_value_rows(value_acc_1, gate_1, 1)
+        row_stats(0)
+        resid_copy(0)
+        row_0 = row_aggr(0)
+        gated_value(value_acc_1, gate_1, 1)
+        selection_times(sel_shift, SHIFT, 0)
+        selection_times(sel_shift, SHIFT, 1)
+        for j in range(PAIRS):
+            for n in range(VARS):
+                nc.tensor.matmul(
+                    out=shift_rows[:, j, :],
+                    lhsT=sel_shift[:, n, j * HALVES : (j + 1) * HALVES, :].rearrange("p h b -> p (h b)"),
+                    rhs=ident_f[:], is_transpose=True, start=(n == 0), stop=(n == VARS - 1),
+                )
         rstd_0 = one_over_std(row_0, 0)
         weighted_0 = centred_times_gain(row_0, 0)
-        residual_stats(gv_rows_1, 1)
-        row_1 = row_statistics(1)
+        row_stats(1)
+        resid_copy(1)
+        row_1 = row_aggr(1)
         total_0 = scaled_plus(weighted_0, rstd_0, shift_rows[:].rearrange("p j q -> p (j q)"), 0)
         rstd_1 = one_over_std(row_1, 1)
         weighted_1 = centred_times_gain(row_1, 1)

@@ -22,8 +22,8 @@ PAIRS = CHUNKS // HALVES
 EPS = 1e-5
 FLOPS = 2 * 3 * VARS * BATCH * FEAT * FEAT
 RUN = 4
-VB1, VB4, VB5, GAIN, SHIFT = 0, 1, 2, 3, 4
-SHARE = {"w1_0": 256, "w1_1": 288, "w4_0": 288, "w4_1": 288, "w5_0": 288, "w5_1": 288}
+VB1, VB4, VB5 = 0, 1, 2
+SHARE = {"w1_0": 256, "w1_1": 288, "w4_0": 288, "w4_1": 288, "w5_0": 288, "w5_1": 256}
 
 
 def tile_variableselectionnetwork_pb_s_kernel(
@@ -33,7 +33,7 @@ def tile_variableselectionnetwork_pb_s_kernel(
     with ExitStack() as stack:
         keep = stack.enter_context(tc.tile_pool(name="keep", bufs=1))
         short_ps = stack.enter_context(tc.psum_pool(name="short_ps", bufs=1))
-        acc_ps = stack.enter_context(tc.psum_pool(name="acc_ps", bufs=2))
+        acc_ps = stack.enter_context(tc.psum_pool(name="acc_ps", bufs=3))
         keep_ps = stack.enter_context(tc.psum_pool(name="keep_ps", bufs=1))
         stack.enter_context(tc.manual_schedule())
 
@@ -66,52 +66,84 @@ def tile_variableselectionnetwork_pb_s_kernel(
             return raw
 
         raw = {"w1_0": load_weight(vW1[0, :, :], "w1_0", 2)}
-        vectors = {VB1: vb1, VB4: vb4, VB5: vb5, GAIN: vlng, SHIFT: vlnb}
+        vectors = {VB1: vb1, VB4: vb4, VB5: vb5}
         for place, vector in vectors.items():
             nc.sync.dma_start(out=vec_rows[VARS * place : VARS * (place + 1), :], in_=vector)
         raw["w1_1"] = load_weight(vW1[1, :, :], "w1_1")
         raw["w4_0"] = load_weight(vW4[0, :, :], "w4_0")
         raw["w4_1"] = load_weight(vW4[1, :, :], "w4_1")
+
+        def load_rows(source, label):
+            rows_sb = keep.tile([P, VARS, PAIRS, P], BF16, name="rows_%s" % label)
+            halves = source.rearrange("b n (j h q) -> h b n j q", h=HALVES, q=P)
+            for h in range(HALVES):
+                nc.sync.dma_start(out=rows_sb[h * BATCH : (h + 1) * BATCH], in_=halves[h])
+            return rows_sb
+
+        def load_spread(vector, label):
+            spread = keep.tile([P, VARS, PAIRS, P], BF16, name="spread_%s" % label)
+            halves = vector.rearrange("n (j h q) -> h n j q", h=HALVES, q=P)
+            for h in range(HALVES):
+                nc.sync.dma_start(out=spread[h * BATCH : (h + 1) * BATCH], in_=halves[h].partition_broadcast(BATCH))
+            return spread
+
+        x_rows = load_rows(x, "x")
         raw["w5_0"] = load_weight(vW5[0, :, :], "w5_0")
         raw["w5_1"] = load_weight(vW5[1, :, :], "w5_1")
-        x_rows = keep.tile([P, VARS, PAIRS, P], BF16)
-        x_halves = x.rearrange("b n (j h q) -> h b n j q", h=HALVES, q=P)
-        for h in range(HALVES):
-            nc.sync.dma_start(out=x_rows[h * BATCH : (h + 1) * BATCH], in_=x_halves[h])
-        sel_sb = keep.tile([P, FEAT], BF16)
-        nc.sync.dma_start(out=sel_sb[:], in_=sel_w.rearrange("b n f -> (b n) f"))
+        sel_rows = load_rows(sel_w, "sel")
+        gain_spread = load_spread(vlng, "gain")
+        shift_spread = load_spread(vlnb, "shift")
 
         one = keep.tile([P, 1], F32)
         nc.vector.memset(one[:], 1.0)
+        minus_half = keep.tile([P, VARS], F32)
+        nc.vector.memset(minus_half[:], -0.5)
+        eps_cols = keep.tile([P, VARS, 2], F32)
+        nc.vector.memset(eps_cols[:], 0.0)
+        nc.vector.memset(eps_cols[:, :, 1], EPS)
         warm = keep.tile([P, 2], F32)
         nc.scalar.activation(out=warm[:, 0:1], in_=one[:], func=ACT.Sigmoid)
 
         grouped = {}
 
-        def regroup(label):
-            g = keep.tile([P, FEAT, PACK], BF16, name="grouped_%s" % label, align_bytes=64)
+        def views(label):
+            if label not in grouped:
+                grouped[label] = keep.tile([P, FEAT, PACK], BF16, name="grouped_%s" % label, align_bytes=64)
             source = raw[label][:].rearrange("p t (c i) -> p c t i", i=RUN)
-            target = g[:].rearrange("p (c i) t -> p c t i", i=RUN)
-            split = SHARE[label] // RUN
+            target = grouped[label][:].rearrange("p (c i) t -> p c t i", i=RUN)
+            return source, target, SHARE[label] // RUN
+
+        def regroup_s(label):
+            source, target, split = views(label)
             nc.scalar.copy(out=target[:, :split], in_=source[:, :split])
+
+        def regroup_v(label):
+            source, target, split = views(label)
             nc.vector.tensor_copy(out=target[:, split:], in_=source[:, split:])
-            grouped[label] = g
+
+        def regroup(label):
+            regroup_s(label)
+            regroup_v(label)
 
         quantised = {}
 
-        def quantise(label):
-            codes = keep.tile([P, FEAT], U32, name="codes_%s" % label, align_bytes=64)
-            scales = keep.tile([P, FEAT], U8, name="scales_%s" % label, align_bytes=64)
+        def quantise(label, c0=0, c1=FEAT):
+            if label not in quantised:
+                codes = keep.tile([P, FEAT], U32, name="codes_%s" % label, align_bytes=64)
+                scales = keep.tile([P, FEAT], U8, name="scales_%s" % label, align_bytes=64)
+                quantised[label] = (codes, scales)
+            codes, scales = quantised[label]
             nc.vector.quantize_mx(
-                out=codes[:].bitcast(FP8X4), scales=scales[:],
-                in_=grouped[label][:].rearrange("p c t -> p (c t)"),
+                out=codes[:, c0:c1].bitcast(FP8X4), scales=scales[:, c0:c1],
+                in_=grouped[label][:, c0:c1, :].rearrange("p c t -> p (c t)"),
             )
-            quantised[label] = (codes, scales)
 
-        def product(label, codes, scales, n):
+        accs = {}
+
+        def product(label, codes, scales, n, chunks=(0, 1, 2, 3)):
             acc = acc_ps.tile([P, CHUNKS, BATCH], F32, name="acc", tag="acc")
             w_codes, w_scales = quantised[label]
-            for c in range(CHUNKS):
+            for c in chunks:
                 cols = slice(c * P, (c + 1) * P)
                 nc.tensor.matmul_mx(
                     out=acc[:, c, :], lhsT=w_codes[:, cols].bitcast(FP8X4), lhsT_scale=w_scales[:, cols],
@@ -171,88 +203,78 @@ def tile_variableselectionnetwork_pb_s_kernel(
 
         r_ps = [keep_ps.tile([P, PAIRS, P], F32, name="r_ps_%d" % n) for n in range(VARS)]
 
+        def flat(rows_view):
+            return rows_view.rearrange("p j q -> p (j q)")
+
         def x_into_rows(n):
-            nc.tensor.matmul(
-                out=r_ps[n][:].rearrange("p j q -> p (j q)"), lhsT=ident_bf[:],
-                rhs=x_rows[:, n].rearrange("p j q -> p (j q)"), start=True, stop=False,
-            )
+            nc.tensor.matmul(out=flat(r_ps[n][:]), lhsT=ident_bf[:], rhs=flat(x_rows[:, n]), start=True, stop=False)
 
-        def add_rows(rows, by_feature, last):
-            for j in range(PAIRS):
-                nc.tensor.matmul(
-                    out=rows[:, j, :],
-                    lhsT=by_feature[:, j * HALVES : (j + 1) * HALVES, :].rearrange("p h b -> p (h b)"),
-                    rhs=ident_f[:], is_transpose=True, start=False, stop=(last and j == PAIRS - 1),
-                )
+        gvs = [keep.tile([P, CHUNKS, BATCH], F32, name="gv_%d" % n) for n in range(VARS)]
 
-        def to_rows(rows, by_feature):
-            for j in range(PAIRS):
-                nc.tensor.transpose(
-                    rows[:, j, :], by_feature[:, j * HALVES : (j + 1) * HALVES, :].rearrange("p h b -> p (h b)"), ident_f[:]
-                )
-
-        def gated_value(value_acc, gate, n):
-            gv = keep.tile([P, CHUNKS, BATCH], F32, name="gv_%d" % n)
-            for c in range(CHUNKS):
+        def gated_value(value_acc, gate, n, j):
+            for c in (HALVES * j, HALVES * j + 1):
                 nc.vector.scalar_tensor_tensor(
-                    out=gv[:, c, :], in0=value_acc[:, c, :], scalar=per_feature(VB5, n)[:, c : c + 1],
+                    out=gvs[n][:, c, :], in0=value_acc[:, c, :], scalar=per_feature(VB5, n)[:, c : c + 1],
                     in1=gate[:, c, :], op0=ALU.add, op1=ALU.mult,
                 )
-            add_rows(r_ps[n], gv, True)
+
+        def add_rows(n, j, last):
+            nc.tensor.matmul(
+                out=r_ps[n][:, j, :],
+                lhsT=gvs[n][:, j * HALVES : (j + 1) * HALVES, :].rearrange("p h b -> p (h b)"),
+                rhs=ident_f[:], is_transpose=True, start=False, stop=last,
+            )
 
         own = keep.tile([P, VARS, 2], F32)
-        resid = keep.tile([P, VARS, PAIRS * P], F32)
         stats = {}
 
         def row_stats(n):
             stats[n] = keep.tile([P, 6], F32, name="stats_%d" % n)
-            nc.vector.bn_stats(out=stats[n][:], in_=r_ps[n][:].rearrange("p j q -> p (j q)"))
+            nc.vector.bn_stats(out=stats[n][:], in_=flat(r_ps[n][:]))
 
         def row_aggr(n):
             nc.vector.bn_aggr(out=own[:, n, :], in_=stats[n][:])
-            row = short_ps.tile([P, 2], F32, name="row", tag="short")
-            nc.tensor.matmul(out=row[:], lhsT=pair[:], rhs=own[:, n, :], start=True, stop=True)
-            return row
 
-        def resid_copy(n):
-            nc.scalar.copy(out=resid[:, n, :], in_=r_ps[n][:].rearrange("p j q -> p (j q)"))
+        dev = keep.tile([P, VARS], F32)
+        var = keep.tile([P, VARS], F32)
+        rstd = keep.tile([P, VARS], F32)
 
-        def one_over_std(row, n):
-            dev = keep.tile([P, 1], F32, name="dev_%d" % n)
-            nc.vector.tensor_tensor(out=dev[:], in0=own[:, n, 0:1], in1=row[:, 0:1], op=ALU.subtract)
-            var = keep.tile([P, 1], F32, name="var_%d" % n)
+        rows = {}
+
+        def open_row(n, pool, tag):
+            rows[n] = pool.tile([P, 2], F32, name="row_%d" % n, tag=tag)
+            nc.tensor.matmul(out=rows[n][:], lhsT=pair[:], rhs=eps_cols[:, n, :], start=True, stop=False)
+
+        def whole_row(n):
+            nc.tensor.matmul(out=rows[n][:], lhsT=pair[:], rhs=own[:, n, :], start=False, stop=True)
+
+        def one_over_std(n):
+            col = slice(n, n + 1)
+            nc.vector.tensor_tensor(out=dev[:, col], in0=own[:, n, 0:1], in1=rows[n][:, 0:1], op=ALU.subtract)
             nc.vector.scalar_tensor_tensor(
-                out=var[:], in0=dev[:], scalar=dev[:], in1=row[:, 1:2], op0=ALU.mult, op1=ALU.add
+                out=var[:, col], in0=dev[:, col], scalar=dev[:, col], in1=rows[n][:, 1:2], op0=ALU.mult, op1=ALU.add
             )
-            rstd = keep.tile([P, 1], F32, name="rstd_%d" % n)
-            nc.scalar.activation(out=rstd[:], in_=var[:], func=ACT.Abs_reciprocal_sqrt, bias=EPS)
-            return rstd
+            nc.gpsimd.tensor_tensor(out=rstd[:, col], in0=var[:, col], in1=minus_half[:, col], op=ALU.pow)
 
-        sel_t = keep_ps.tile([P, CHUNKS, P], BF16)
-        gain_rows = keep_ps.tile([P, VARS, PAIRS, P], F32)
-        shift_rows = keep_ps.tile([P, PAIRS, P], F32)
-        sel_gain = keep.tile([P, VARS, CHUNKS, BATCH], F32)
-        sel_shift = keep.tile([P, VARS, CHUNKS, BATCH], F32)
+        sel_gain = keep.tile([P, VARS, PAIRS * P], F32)
+        sel_shift = keep.tile([P, VARS, PAIRS * P], F32)
+        shift_sum = keep.tile([P, PAIRS * P], F32)
 
-        def selection_times(target, place, n):
-            for c in range(CHUNKS):
-                nc.scalar.activation(
-                    out=target[:, n, c, :], in_=sel_t[:, c, :].rearrange("p (b n) -> p n b", n=VARS)[:, n, :],
-                    func=ACT.Copy, scale=per_feature(place, n)[:, c : c + 1],
-                )
+        def selection_times(target, spread, n):
+            nc.gpsimd.tensor_tensor(out=target[:, n, :], in0=flat(sel_rows[:, n]), in1=flat(spread[:, n]), op=ALU.mult)
 
-        def centred_times_gain(row, n):
+        def centred_times_gain(n):
             weighted = keep.tile([P, PAIRS * P], F32, name="weighted_%d" % n)
             nc.vector.scalar_tensor_tensor(
-                out=weighted[:], in0=resid[:, n, :], scalar=row[:, 0:1],
-                in1=gain_rows[:, n].rearrange("p j q -> p (j q)"), op0=ALU.subtract, op1=ALU.mult,
+                out=weighted[:], in0=flat(r_ps[n][:]), scalar=rows[n][:, 0:1], in1=sel_gain[:, n, :],
+                op0=ALU.subtract, op1=ALU.mult,
             )
             return weighted
 
-        def scaled_plus(weighted, rstd, addend, n):
+        def scaled_plus(weighted, addend, n):
             summed = keep.tile([P, PAIRS * P], F32, name="summed_%d" % n)
             nc.vector.scalar_tensor_tensor(
-                out=summed[:], in0=weighted[:], scalar=rstd[:], in1=addend, op0=ALU.mult, op1=ALU.add
+                out=summed[:], in0=weighted[:], scalar=rstd[:, n : n + 1], in1=addend, op0=ALU.mult, op1=ALU.add
             )
             return summed[:]
 
@@ -265,58 +287,57 @@ def tile_variableselectionnetwork_pb_s_kernel(
         quantise("w1_1")
         e1_acc_1 = product("w1_1", hv_codes, hv_scales, 1)
         e1_add(e1_acc_0, 0)
+        open_row(0, short_ps, "short")
+        open_row(1, keep_ps, "row_1")
 
         regroup("w4_1")
         e1_quantise(0)
         quantise("w4_0")
         gate_acc_0 = product("w4_0", e1_codes, e1_scales, 0)
         e1_add(e1_acc_1, 1)
-        for n in range(VARS):
-            x_into_rows(n)
-        for c in range(CHUNKS):
-            nc.tensor.transpose(sel_t[:, c, :], sel_sb[:, c * P : (c + 1) * P], ident_bf[:])
 
         regroup("w5_0")
         e1_quantise(1)
         quantise("w4_1")
         gate_acc_1 = product("w4_1", e1_codes, e1_scales, 1)
-        gate_0 = sigmoid(gate_acc_0, 0)
-        selection_times(sel_gain, GAIN, 0)
-        selection_times(sel_gain, GAIN, 1)
-        to_rows(gain_rows[:, 0], sel_gain[:, 0])
-        to_rows(gain_rows[:, 1], sel_gain[:, 1])
+        for n in range(VARS):
+            x_into_rows(n)
 
         regroup("w5_1")
         quantise("w5_0")
         value_acc_0 = product("w5_0", e1_codes, e1_scales, 0)
+        gate_0 = sigmoid(gate_acc_0, 0)
         gate_1 = sigmoid(gate_acc_1, 1)
-        gated_value(value_acc_0, gate_0, 0)
-        quantise("w5_1")
-        value_acc_1 = product("w5_1", e1_codes, e1_scales, 1)
+        quantise("w5_1", 256, 512)
+        value_acc_1b = product("w5_1", e1_codes, e1_scales, 1, (2, 3))
+        quantise("w5_1", 0, 256)
+        value_acc_1a = product("w5_1", e1_codes, e1_scales, 1, (0, 1))
+        for n in range(VARS):
+            selection_times(sel_gain, gain_spread, n)
+        for n in range(VARS):
+            selection_times(sel_shift, shift_spread, n)
+        nc.gpsimd.tensor_tensor(out=shift_sum[:], in0=sel_shift[:, 0, :], in1=sel_shift[:, 1, :], op=ALU.add)
 
-        nc.scalar.activation(out=warm[:, 1:2], in_=one[:], func=ACT.Abs_reciprocal_sqrt)
+        gated_value(value_acc_0, gate_0, 0, 0)
+        add_rows(0, 0, False)
+        gated_value(value_acc_0, gate_0, 0, 1)
+        add_rows(0, 1, True)
+        gated_value(value_acc_1b, gate_1, 1, 1)
+        add_rows(1, 1, False)
+        gated_value(value_acc_1a, gate_1, 1, 0)
+        add_rows(1, 0, True)
         row_stats(0)
-        resid_copy(0)
-        row_0 = row_aggr(0)
-        gated_value(value_acc_1, gate_1, 1)
-        selection_times(sel_shift, SHIFT, 0)
-        selection_times(sel_shift, SHIFT, 1)
-        for j in range(PAIRS):
-            for n in range(VARS):
-                nc.tensor.matmul(
-                    out=shift_rows[:, j, :],
-                    lhsT=sel_shift[:, n, j * HALVES : (j + 1) * HALVES, :].rearrange("p h b -> p (h b)"),
-                    rhs=ident_f[:], is_transpose=True, start=(n == 0), stop=(n == VARS - 1),
-                )
-        rstd_0 = one_over_std(row_0, 0)
-        weighted_0 = centred_times_gain(row_0, 0)
+        row_aggr(0)
+        whole_row(0)
         row_stats(1)
-        resid_copy(1)
-        row_1 = row_aggr(1)
-        total_0 = scaled_plus(weighted_0, rstd_0, shift_rows[:].rearrange("p j q -> p (j q)"), 0)
-        rstd_1 = one_over_std(row_1, 1)
-        weighted_1 = centred_times_gain(row_1, 1)
-        total = scaled_plus(weighted_1, rstd_1, total_0, 1)
+        row_aggr(1)
+        whole_row(1)
+        one_over_std(0)
+        weighted_0 = centred_times_gain(0)
+        total_0 = scaled_plus(weighted_0, shift_sum[:], 0)
+        one_over_std(1)
+        weighted_1 = centred_times_gain(1)
+        total = scaled_plus(weighted_1, total_0, 1)
 
         out_halves = out.rearrange("b (j h q) -> h b j q", h=HALVES, q=P)
         result = total.rearrange("p (j q) -> p j q", q=P)

@@ -22,7 +22,7 @@ PAIRS = CHUNKS // HALVES
 EPS = 1e-5
 FLOPS = 2 * 3 * VARS * BATCH * FEAT * FEAT
 RUN = 4
-VB1, VB4, VB5 = 0, 1, 2
+VB4, VB5 = 0, 1
 SHARE = {"w1_0": 256, "w1_1": 288, "w4_0": 288, "w4_1": 288, "w5_0": 288, "w5_1": 256}
 
 
@@ -56,17 +56,15 @@ def tile_variableselectionnetwork_pb_s_kernel(
         hv_sb = keep.tile([P, FEAT], BF16)
         nc.sync.dma_start(out=hv_sb[:], in_=hv.rearrange("b n k -> (b n) k"))
 
-        def load_weight(weight, label, pieces=1):
+        def load_weight(weight, label):
             raw = keep.tile([P, PACK, FEAT], BF16, name="raw_%s" % label)
-            view = weight.rearrange("(t p) c -> p t c", p=P)
-            width = FEAT // pieces
-            for i in range(pieces):
-                cols = slice(i * width, (i + 1) * width)
-                nc.sync.dma_start(out=raw[:, :, cols], in_=view[:, :, cols])
+            nc.sync.dma_start(out=raw[:], in_=weight.rearrange("(p t) c -> p t c", t=PACK))
             return raw
 
-        raw = {"w1_0": load_weight(vW1[0, :, :], "w1_0", 2)}
-        vectors = {VB1: vb1, VB4: vb4, VB5: vb5}
+        raw = {"w1_0": load_weight(vW1[0, :, :], "w1_0")}
+        vb1_sb = keep.tile([P, VARS, PACK], BF16)
+        nc.sync.dma_start(out=vb1_sb[:], in_=vb1.rearrange("n (p t) -> p n t", t=PACK))
+        vectors = {VB4: vb4, VB5: vb5}
         for place, vector in vectors.items():
             nc.sync.dma_start(out=vec_rows[VARS * place : VARS * (place + 1), :], in_=vector)
         raw["w1_1"] = load_weight(vW1[1, :, :], "w1_1")
@@ -87,9 +85,9 @@ def tile_variableselectionnetwork_pb_s_kernel(
                 nc.sync.dma_start(out=spread[h * BATCH : (h + 1) * BATCH], in_=halves[h].partition_broadcast(BATCH))
             return spread
 
-        x_rows = load_rows(x, "x")
         raw["w5_0"] = load_weight(vW5[0, :, :], "w5_0")
         raw["w5_1"] = load_weight(vW5[1, :, :], "w5_1")
+        x_rows = load_rows(x, "x")
         sel_rows = load_rows(sel_w, "sel")
         gain_spread = load_spread(vlng, "gain")
         shift_spread = load_spread(vlnb, "shift")
@@ -110,7 +108,10 @@ def tile_variableselectionnetwork_pb_s_kernel(
             if label not in grouped:
                 grouped[label] = keep.tile([P, FEAT, PACK], BF16, name="grouped_%s" % label, align_bytes=64)
             source = raw[label][:].rearrange("p t (c i) -> p c t i", i=RUN)
-            target = grouped[label][:].rearrange("p (c i) t -> p c t i", i=RUN)
+            if label.startswith("w1"):
+                target = grouped[label][:].rearrange("p (i c) t -> p c t i", i=RUN)
+            else:
+                target = grouped[label][:].rearrange("p (c i) t -> p c t i", i=RUN)
             return source, target, SHARE[label] // RUN
 
         def regroup_s(label):
@@ -151,11 +152,15 @@ def tile_variableselectionnetwork_pb_s_kernel(
                 )
             return acc
 
-        hv_t = short_ps.tile([P, PACK, P], BF16, tag="short")
-        for t in range(PACK):
-            nc.tensor.transpose(hv_t[:, t, :], hv_sb[:, t * P : (t + 1) * P], ident_bf[:])
+        hv_words = hv_sb[:].bitcast(F32)
+        hv_t = short_ps.tile([P, 2, P], F32, tag="short")
+        for u in range(2):
+            nc.tensor.transpose(hv_t[:, u, :], hv_words[:, u : FEAT // 2 : 2], ident_f[:])
         hv_grouped = keep.tile([P, VARS, BATCH, PACK], BF16, align_bytes=64)
-        nc.scalar.copy(out=hv_grouped[:], in_=hv_t[:].rearrange("p t (b n) -> p n b t", n=VARS))
+        nc.scalar.copy(
+            out=hv_grouped[:].rearrange("p n b t -> p (n b t)").bitcast(F32).rearrange("p (n b u) -> p n b u", n=VARS, u=2),
+            in_=hv_t[:].rearrange("p u (b n) -> p n b u", n=VARS),
+        )
         hv_codes = keep.tile([P, VARS, BATCH], U32, align_bytes=64)
         hv_scales = keep.tile([P, VARS, BATCH], U8, align_bytes=64)
 
@@ -182,7 +187,7 @@ def tile_variableselectionnetwork_pb_s_kernel(
             g = keep.tile([P, BATCH, PACK], BF16, name="e1_grouped_%d" % n, align_bytes=64)
             nc.vector.tensor_tensor(
                 out=g[:], in0=e1_acc[:].rearrange("p c b -> p b c"),
-                in1=per_feature(VB1, n).unsqueeze(1).to_broadcast([P, BATCH, PACK]), op=ALU.add,
+                in1=vb1_sb[:, n, :].unsqueeze(1).to_broadcast([P, BATCH, PACK]), op=ALU.add,
             )
             e1_grouped[n] = g
 

@@ -62,14 +62,14 @@ def tile_variableselectionnetwork_pb_s_kernel(
             return raw
 
         raw = {"w1_0": load_weight(vW1[0, :, :], "w1_0")}
+        raw["w1_1"] = load_weight(vW1[1, :, :], "w1_1")
+        raw["w4_0"] = load_weight(vW4[0, :, :], "w4_0")
         vb1_sb = keep.tile([P, VARS, PACK], BF16)
         nc.sync.dma_start(out=vb1_sb[:], in_=vb1.rearrange("n (p t) -> p n t", t=PACK))
+        raw["w4_1"] = load_weight(vW4[1, :, :], "w4_1")
         vectors = {VB4: vb4, VB5: vb5}
         for place, vector in vectors.items():
             nc.sync.dma_start(out=vec_rows[VARS * place : VARS * (place + 1), :], in_=vector)
-        raw["w1_1"] = load_weight(vW1[1, :, :], "w1_1")
-        raw["w4_0"] = load_weight(vW4[0, :, :], "w4_0")
-        raw["w4_1"] = load_weight(vW4[1, :, :], "w4_1")
 
         def load_rows(source, label):
             rows_sb = keep.tile([P, VARS, PAIRS, P], BF16, name="rows_%s" % label)
@@ -94,8 +94,6 @@ def tile_variableselectionnetwork_pb_s_kernel(
 
         one = keep.tile([P, 1], F32)
         nc.vector.memset(one[:], 1.0)
-        minus_half = keep.tile([P, VARS], F32)
-        nc.vector.memset(minus_half[:], -0.5)
         eps_cols = keep.tile([P, VARS, 2], F32)
         nc.vector.memset(eps_cols[:], 0.0)
         nc.vector.memset(eps_cols[:, :, 1], EPS)
@@ -141,8 +139,9 @@ def tile_variableselectionnetwork_pb_s_kernel(
 
         accs = {}
 
-        def product(label, codes, scales, n, chunks=(0, 1, 2, 3)):
-            acc = acc_ps.tile([P, CHUNKS, BATCH], F32, name="acc", tag="acc")
+        def product(label, codes, scales, n, chunks=(0, 1, 2, 3), acc=None):
+            if acc is None:
+                acc = acc_ps.tile([P, CHUNKS, BATCH], F32, name="acc", tag="acc")
             w_codes, w_scales = quantised[label]
             for c in chunks:
                 cols = slice(c * P, (c + 1) * P)
@@ -171,30 +170,35 @@ def tile_variableselectionnetwork_pb_s_kernel(
             in_=hv_grouped[:].rearrange("p n b t -> p (n b t)"),
         )
 
-        vec_t = short_ps.tile([P, CHUNKS, P], BF16, tag="short")
-        for c in range(CHUNKS):
-            nc.tensor.transpose(vec_t[:, c, :], vec_rows[:, c * P : (c + 1) * P], ident_bf[:])
+        vec_t = keep_ps.tile([P, CHUNKS, P], BF16)
         vecs = keep.tile([P, len(vectors) * VARS, CHUNKS], F32)
+
+        def transpose_vectors():
+            for c in range(CHUNKS):
+                nc.tensor.transpose(vec_t[:, c, :], vec_rows[:, c * P : (c + 1) * P], ident_bf[:])
+
+        def copy_vectors():
+            nc.scalar.copy(out=vecs[:], in_=vec_t[:, :, : len(vectors) * VARS].rearrange("p c r -> p r c"))
 
         def per_feature(place, n):
             return vecs[:, VARS * place + n, :]
 
         e1_codes = keep.tile([P, VARS, BATCH], U32, align_bytes=64)
         e1_scales = keep.tile([P, VARS, BATCH], U8, align_bytes=64)
-        e1_grouped = {}
+        e1_acc = acc_ps.tile([P, VARS, CHUNKS, BATCH], F32, name="acc", tag="acc")
+        e1_grouped = keep.tile([P, VARS, BATCH, PACK], BF16, align_bytes=64)
 
-        def e1_add(e1_acc, n):
-            g = keep.tile([P, BATCH, PACK], BF16, name="e1_grouped_%d" % n, align_bytes=64)
+        def e1_add():
             nc.vector.tensor_tensor(
-                out=g[:], in0=e1_acc[:].rearrange("p c b -> p b c"),
-                in1=vb1_sb[:, n, :].unsqueeze(1).to_broadcast([P, BATCH, PACK]), op=ALU.add,
+                out=e1_grouped[:], in0=e1_acc[:].rearrange("p n c b -> p n b c"),
+                in1=vb1_sb[:].unsqueeze(2).to_broadcast([P, VARS, BATCH, PACK]), op=ALU.add,
             )
-            e1_grouped[n] = g
 
-        def e1_quantise(n):
+        def e1_quantise():
             nc.vector.quantize_mx(
-                out=e1_codes[:, n, :].bitcast(FP8X4), scales=e1_scales[:, n, :],
-                in_=e1_grouped[n][:].rearrange("p b c -> p (b c)"),
+                out=e1_codes[:].rearrange("p n b -> p (n b)").bitcast(FP8X4),
+                scales=e1_scales[:].rearrange("p n b -> p (n b)"),
+                in_=e1_grouped[:].rearrange("p n b c -> p (n b c)"),
             )
 
         def sigmoid(gate_acc, n):
@@ -241,7 +245,6 @@ def tile_variableselectionnetwork_pb_s_kernel(
             nc.vector.bn_aggr(out=own[:, n, :], in_=stats[n][:])
 
         dev = keep.tile([P, VARS], F32)
-        var = keep.tile([P, VARS], F32)
         rstd = keep.tile([P, VARS], F32)
 
         rows = {}
@@ -255,11 +258,8 @@ def tile_variableselectionnetwork_pb_s_kernel(
 
         def one_over_std(n):
             col = slice(n, n + 1)
-            nc.vector.tensor_tensor(out=dev[:, col], in0=own[:, n, 0:1], in1=rows[n][:, 0:1], op=ALU.subtract)
-            nc.vector.scalar_tensor_tensor(
-                out=var[:, col], in0=dev[:, col], scalar=dev[:, col], in1=rows[n][:, 1:2], op0=ALU.mult, op1=ALU.add
-            )
-            nc.gpsimd.tensor_tensor(out=rstd[:, col], in0=var[:, col], in1=minus_half[:, col], op=ALU.pow)
+            nc.scalar.activation(out=dev[:, col], in_=rows[n][:, 0:1], func=ACT.Square, scale=-1.0, bias=own[:, n, 0:1])
+            nc.scalar.activation(out=rstd[:, col], in_=rows[n][:, 1:2], func=ACT.Abs_reciprocal_sqrt, bias=dev[:, col])
 
         sel_gain = keep.tile([P, VARS, PAIRS * P], F32)
         sel_shift = keep.tile([P, VARS, PAIRS * P], F32)
@@ -285,24 +285,23 @@ def tile_variableselectionnetwork_pb_s_kernel(
 
         regroup("w1_1")
         quantise("w1_0")
-        e1_acc_0 = product("w1_0", hv_codes, hv_scales, 0)
-        nc.vector.tensor_copy(out=vecs[:], in_=vec_t[:, :, : len(vectors) * VARS].rearrange("p c r -> p r c"))
+        product("w1_0", hv_codes, hv_scales, 0, acc=e1_acc[:, 0])
 
         regroup("w4_0")
         quantise("w1_1")
-        e1_acc_1 = product("w1_1", hv_codes, hv_scales, 1)
-        e1_add(e1_acc_0, 0)
+        product("w1_1", hv_codes, hv_scales, 1, acc=e1_acc[:, 1])
+        transpose_vectors()
         open_row(0, short_ps, "short")
         open_row(1, keep_ps, "row_1")
 
         regroup("w4_1")
-        e1_quantise(0)
         quantise("w4_0")
-        gate_acc_0 = product("w4_0", e1_codes, e1_scales, 0)
-        e1_add(e1_acc_1, 1)
+        e1_add()
 
+        copy_vectors()
         regroup("w5_0")
-        e1_quantise(1)
+        e1_quantise()
+        gate_acc_0 = product("w4_0", e1_codes, e1_scales, 0)
         quantise("w4_1")
         gate_acc_1 = product("w4_1", e1_codes, e1_scales, 1)
         for n in range(VARS):
@@ -313,6 +312,7 @@ def tile_variableselectionnetwork_pb_s_kernel(
         value_acc_0 = product("w5_0", e1_codes, e1_scales, 0)
         gate_0 = sigmoid(gate_acc_0, 0)
         gate_1 = sigmoid(gate_acc_1, 1)
+        nc.scalar.activation(out=warm[:, 1:2], in_=one[:], func=ACT.Abs_reciprocal_sqrt)
         quantise("w5_1", 256, 512)
         value_acc_1b = product("w5_1", e1_codes, e1_scales, 1, (2, 3))
         quantise("w5_1", 0, 256)
@@ -338,10 +338,10 @@ def tile_variableselectionnetwork_pb_s_kernel(
         row_aggr(1)
         whole_row(1)
         one_over_std(0)
-        weighted_0 = centred_times_gain(0)
-        total_0 = scaled_plus(weighted_0, shift_sum[:], 0)
         one_over_std(1)
+        weighted_0 = centred_times_gain(0)
         weighted_1 = centred_times_gain(1)
+        total_0 = scaled_plus(weighted_0, shift_sum[:], 0)
         total = scaled_plus(weighted_1, total_0, 1)
 
         out_halves = out.rearrange("b (j h q) -> h b j q", h=HALVES, q=P)

@@ -265,8 +265,11 @@ def tile_variableselectionnetwork_pb_s_kernel(
         sel_shift = keep.tile([P, VARS, PAIRS * P], F32)
         shift_sum = keep.tile([P, PAIRS * P], F32)
 
-        def selection_times(target, spread, n):
-            nc.gpsimd.tensor_tensor(out=target[:, n, :], in0=flat(sel_rows[:, n]), in1=flat(spread[:, n]), op=ALU.mult)
+        def selection_times(target, spread):
+            nc.gpsimd.tensor_tensor(
+                out=target[:].rearrange("p n f -> p (n f)"), in0=sel_rows[:].rearrange("p n j q -> p (n j q)"),
+                in1=spread[:].rearrange("p n j q -> p (n j q)"), op=ALU.mult,
+            )
 
         def centred_times_gain(n):
             weighted = keep.tile([P, PAIRS * P], F32, name="weighted_%d" % n)
@@ -317,11 +320,8 @@ def tile_variableselectionnetwork_pb_s_kernel(
         value_acc_1b = product("w5_1", e1_codes, e1_scales, 1, (2, 3))
         quantise("w5_1", 0, 256)
         value_acc_1a = product("w5_1", e1_codes, e1_scales, 1, (0, 1))
-        for n in range(VARS):
-            selection_times(sel_gain, gain_spread, n)
-        for n in range(VARS):
-            selection_times(sel_shift, shift_spread, n)
-        nc.gpsimd.tensor_tensor(out=shift_sum[:], in0=sel_shift[:, 0, :], in1=sel_shift[:, 1, :], op=ALU.add)
+        nc.vector.tensor_copy(out=sel_rows[:, 0, 0, 0:1], in_=sel_rows[:, 0, 0, 0:1])
+        selection_times(sel_gain, gain_spread)
 
         gated_value(value_acc_0, gate_0, 0, 0)
         add_rows(0, 0, False)
@@ -332,14 +332,17 @@ def tile_variableselectionnetwork_pb_s_kernel(
         gated_value(value_acc_1a, gate_1, 1, 0)
         add_rows(1, 0, True)
         row_stats(0)
+        nc.vector.tensor_tensor(out=sel_shift[:, 0, :], in0=flat(sel_rows[:, 0]), in1=flat(shift_spread[:, 0]), op=ALU.mult)
         row_aggr(0)
         whole_row(0)
         row_stats(1)
+        nc.vector.tensor_tensor(out=sel_shift[:, 1, :], in0=flat(sel_rows[:, 1]), in1=flat(shift_spread[:, 1]), op=ALU.mult)
         row_aggr(1)
         whole_row(1)
         one_over_std(0)
         one_over_std(1)
         weighted_0 = centred_times_gain(0)
+        nc.vector.tensor_tensor(out=shift_sum[:], in0=sel_shift[:, 0, :], in1=sel_shift[:, 1, :], op=ALU.add)
         weighted_1 = centred_times_gain(1)
         total_0 = scaled_plus(weighted_0, shift_sum[:], 0)
         total = scaled_plus(weighted_1, total_0, 1)

@@ -322,6 +322,7 @@ def tile_variableselectionnetwork_pb_s_kernel(
         value_acc_1a = product("w5_1", e1_codes, e1_scales, 1, (0, 1))
         nc.vector.tensor_copy(out=sel_rows[:, 0, 0, 0:1], in_=sel_rows[:, 0, 0, 0:1])
         selection_times(sel_gain, gain_spread)
+        selection_times(sel_shift, shift_spread)
 
         gated_value(value_acc_0, gate_0, 0, 0)
         add_rows(0, 0, False)
@@ -332,11 +333,9 @@ def tile_variableselectionnetwork_pb_s_kernel(
         gated_value(value_acc_1a, gate_1, 1, 0)
         add_rows(1, 0, True)
         row_stats(0)
-        nc.vector.tensor_tensor(out=sel_shift[:, 0, :], in0=flat(sel_rows[:, 0]), in1=flat(shift_spread[:, 0]), op=ALU.mult)
         row_aggr(0)
         whole_row(0)
         row_stats(1)
-        nc.vector.tensor_tensor(out=sel_shift[:, 1, :], in0=flat(sel_rows[:, 1]), in1=flat(shift_spread[:, 1]), op=ALU.mult)
         row_aggr(1)
         whole_row(1)
         one_over_std(0)

@@ -323,6 +323,7 @@ def tile_variableselectionnetwork_pb_s_kernel(
         nc.vector.tensor_copy(out=sel_rows[:, 0, 0, 0:1], in_=sel_rows[:, 0, 0, 0:1])
         selection_times(sel_gain, gain_spread)
         selection_times(sel_shift, shift_spread)
+        nc.gpsimd.tensor_tensor(out=shift_sum[:], in0=sel_shift[:, 0, :], in1=sel_shift[:, 1, :], op=ALU.add)
 
         gated_value(value_acc_0, gate_0, 0, 0)
         add_rows(0, 0, False)
@@ -341,7 +342,6 @@ def tile_variableselectionnetwork_pb_s_kernel(
         one_over_std(0)
         one_over_std(1)
         weighted_0 = centred_times_gain(0)
-        nc.vector.tensor_tensor(out=shift_sum[:], in0=sel_shift[:, 0, :], in1=sel_shift[:, 1, :], op=ALU.add)
         weighted_1 = centred_times_gain(1)
         total_0 = scaled_plus(weighted_0, shift_sum[:], 0)
         total = scaled_plus(weighted_1, total_0, 1)

from contextlib import ExitStack

import concourse.mybir as mybir
from concourse.masks import make_identity

F32 = mybir.dt.float32
BF16 = mybir.dt.bfloat16
U32 = mybir.dt.uint32
U8 = mybir.dt.uint8
FP8X4 = mybir.dt.float8_e4m3fn_x4
ALU = mybir.AluOpType
ACT = mybir.ActivationFunctionType

P = 128
PACK = 4
BATCH = 64
VARS = 2
FEAT = 512
CHUNKS = FEAT // P
HALVES = P // BATCH
PAIRS = CHUNKS // HALVES
EPS = 1e-5
FLOPS = 2 * 3 * VARS * BATCH * FEAT * FEAT
RUN = 4
VB4, VB5 = 0, 1
SHARE = {"w1_0": 256, "w1_1": 288, "w4_0": 288, "w4_1": 288, "w5_0": 288, "w5_1": 256}


def tile_variableselectionnetwork_pb_s_kernel(
    tc, hv, x, sel_w, vW1, vb1, vW4, vb4, vW5, vb5, vlng, vlnb, out
):
    nc = tc.nc
    with ExitStack() as stack:
        keep = stack.enter_context(tc.tile_pool(name="keep", bufs=1))
        short_ps = stack.enter_context(tc.psum_pool(name="short_ps", bufs=1))
        acc_ps = stack.enter_context(tc.psum_pool(name="acc_ps", bufs=3))
        keep_ps = stack.enter_context(tc.psum_pool(name="keep_ps", bufs=1))
        stack.enter_context(tc.manual_schedule())

        vec_rows = keep.tile([P, FEAT], BF16)
        nc.vector.memset(vec_rows[:], 0.0)
        ident_bf = keep.tile([P, P], BF16)
        nc.vector.memset(ident_bf[:], 0.0)
        make_identity(nc, ident_bf[:], nomemset=True)
        ident_f = keep.tile([P, P], F32)
        nc.vector.memset(ident_f[:], 0.0)
        make_identity(nc, ident_f[:], nomemset=True)
        pair = keep.tile([P, P], F32)
        nc.vector.memset(pair[:], 0.0)
        for base in (0, BATCH, -BATCH):
            nc.gpsimd.affine_select(
                out=pair[:], in_=pair[:], compare_op=ALU.not_equal, fill=1.0 / HALVES, base=base,
                pattern=[[-1, P]], channel_multiplier=1,
            )

        hv_sb = keep.tile([P, FEAT], BF16)
        nc.sync.dma_start(out=hv_sb[:], in_=hv.rearrange("b n k -> (b n) k"))

        def load_weight(weight, label):
            raw = keep.tile([P, PACK, FEAT], BF16, name="raw_%s" % label)
            nc.sync.dma_start(out=raw[:], in_=weight.rearrange("(p t) c -> p t c", t=PACK))
            return raw

        raw = {"w1_0": load_weight(vW1[0, :, :], "w1_0")}
        raw["w1_1"] = load_weight(vW1[1, :, :], "w1_1")
        raw["w4_0"] = load_weight(vW4[0, :, :], "w4_0")
        vb1_sb = keep.tile([P, VARS, PACK], BF16)
        nc.sync.dma_start(out=vb1_sb[:], in_=vb1.rearrange("n (p t) -> p n t", t=PACK))
        raw["w4_1"] = load_weight(vW4[1, :, :], "w4_1")
        vectors = {VB4: vb4, VB5: vb5}
        for place, vector in vectors.items():
            nc.sync.dma_start(out=vec_rows[VARS * place : VARS * (place + 1), :], in_=vector)

        def load_rows(source, label):
            rows_sb = keep.tile([P, VARS, PAIRS, P], BF16, name="rows_%s" % label)
            halves = source.rearrange("b n (j h q) -> h b n j q", h=HALVES, q=P)
            for h in range(HALVES):
                nc.sync.dma_start(out=rows_sb[h * BATCH : (h + 1) * BATCH], in_=halves[h])
            return rows_sb

        def load_spread(vector, label):
            spread = keep.tile([P, VARS, PAIRS, P], BF16, name="spread_%s" % label)
            halves = vector.rearrange("n (j h q) -> h n j q", h=HALVES, q=P)
            for h in range(HALVES):
                nc.sync.dma_start(out=spread[h * BATCH : (h + 1) * BATCH], in_=halves[h].partition_broadcast(BATCH))
            return spread

        raw["w5_0"] = load_weight(vW5[0, :, :], "w5_0")
        raw["w5_1"] = load_weight(vW5[1, :, :], "w5_1")
        x_rows = load_rows(x, "x")
        sel_rows = load_rows(sel_w, "sel")
        gain_spread = load_spread(vlng, "gain")
        shift_spread = load_spread(vlnb, "shift")

        one = keep.tile([P, 1], F32)
        nc.vector.memset(one[:], 1.0)
        eps_cols = keep.tile([P, VARS, 2], F32)
        nc.vector.memset(eps_cols[:], 0.0)
        nc.vector.memset(eps_cols[:, :, 1], EPS)
        warm = keep.tile([P, 2], F32)
        nc.scalar.activation(out=warm[:, 0:1], in_=one[:], func=ACT.Sigmoid)

        grouped = {}

        def views(label):
            if label not in grouped:
                grouped[label] = keep.tile([P, FEAT, PACK], BF16, name="grouped_%s" % label, align_bytes=64)
            source = raw[label][:].rearrange("p t (c i) -> p c t i", i=RUN)
            if label.startswith("w1"):
                target = grouped[label][:].rearrange("p (i c) t -> p c t i", i=RUN)
            else:
                target = grouped[label][:].rearrange("p (c i) t -> p c t i", i=RUN)
            return source, target, SHARE[label] // RUN

        def regroup_s(label):
            source, target, split = views(label)
            nc.scalar.copy(out=target[:, :split], in_=source[:, :split])

        def regroup_v(label):
            source, target, split = views(label)
            nc.vector.tensor_copy(out=target[:, split:], in_=source[:, split:])

        def regroup(label):
            regroup_s(label)
            regroup_v(label)

        quantised = {}

        def quantise(label, c0=0, c1=FEAT):
            if label not in quantised:
                codes = keep.tile([P, FEAT], U32, name="codes_%s" % label, align_bytes=64)
                scales = keep.tile([P, FEAT], U8, name="scales_%s" % label, align_bytes=64)
                quantised[label] = (codes, scales)
            codes, scales = quantised[label]
            nc.vector.quantize_mx(
                out=codes[:, c0:c1].bitcast(FP8X4), scales=scales[:, c0:c1],
                in_=grouped[label][:, c0:c1, :].rearrange("p c t -> p (c t)"),
            )

        accs = {}

        def product(label, codes, scales, n, chunks=(0, 1, 2, 3), acc=None):
            if acc is None:
                acc = acc_ps.tile([P, CHUNKS, BATCH], F32, name="acc", tag="acc")
            w_codes, w_scales = quantised[label]
            for c in chunks:
                cols = slice(c * P, (c + 1) * P)
                nc.tensor.matmul_mx(
                    out=acc[:, c, :], lhsT=w_codes[:, cols].bitcast(FP8X4), lhsT_scale=w_scales[:, cols],
                    rhs=codes[:, n, :].bitcast(FP8X4), rhs_scale=scales[:, n, :], start=True, stop=True,
                )
            return acc

        hv_words = hv_sb[:].bitcast(F32)
        hv_t = short_ps.tile([P, 2, P], F32, tag="short")
        for u in range(2):
            nc.tensor.transpose(hv_t[:, u, :], hv_words[:, u : FEAT // 2 : 2], ident_f[:])
        hv_grouped = keep.tile([P, VARS, BATCH, PACK], BF16, align_bytes=64)
        nc.scalar.copy(
            out=hv_grouped[:].rearrange("p n b t -> p (n b t)").bitcast(F32).rearrange("p (n b u) -> p n b u", n=VARS, u=2),
            in_=hv_t[:].rearrange("p u (b n) -> p n b u", n=VARS),
        )
        hv_codes = keep.tile([P, VARS, BATCH], U32, align_bytes=64)
        hv_scales = keep.tile([P, VARS, BATCH], U8, align_bytes=64)

        regroup("w1_0")
        nc.vector.quantize_mx(
            out=hv_codes[:].rearrange("p n b -> p (n b)").bitcast(FP8X4),
            scales=hv_scales[:].rearrange("p n b -> p (n b)"),
            in_=hv_grouped[:].rearrange("p n b t -> p (n b t)"),
        )

        vec_t = keep_ps.tile([P, CHUNKS, P], BF16)
        vecs = keep.tile([P, len(vectors) * VARS, CHUNKS], F32)

        def transpose_vectors():
            for c in range(CHUNKS):
                nc.tensor.transpose(vec_t[:, c, :], vec_rows[:, c * P : (c + 1) * P], ident_bf[:])

        def copy_vectors():
            nc.scalar.copy(out=vecs[:], in_=vec_t[:, :, : len(vectors) * VARS].rearrange("p c r -> p r c"))

        def per_feature(place, n):
            return vecs[:, VARS * place + n, :]

        e1_codes = keep.tile([P, VARS, BATCH], U32, align_bytes=64)
        e1_scales = keep.tile([P, VARS, BATCH], U8, align_bytes=64)
        e1_acc = acc_ps.tile([P, VARS, CHUNKS, BATCH], F32, name="acc", tag="acc")
        e1_grouped = keep.tile([P, VARS, BATCH, PACK], BF16, align_bytes=64)

        def e1_add():
            nc.vector.tensor_tensor(
                out=e1_grouped[:], in0=e1_acc[:].rearrange("p n c b -> p n b c"),
                in1=vb1_sb[:].unsqueeze(2).to_broadcast([P, VARS, BATCH, PACK]), op=ALU.add,
            )

        def e1_quantise():
            nc.vector.quantize_mx(
                out=e1_codes[:].rearrange("p n b -> p (n b)").bitcast(FP8X4),
                scales=e1_scales[:].rearrange("p n b -> p (n b)"),
                in_=e1_grouped[:].rearrange("p n b c -> p (n b c)"),
            )

        def sigmoid(gate_acc, n):
            gate = keep.tile([P, CHUNKS, BATCH], F32, name="gate_%d" % n)
            for c in range(CHUNKS):
                nc.scalar.activation(
                    out=gate[:, c, :], in_=gate_acc[:, c, :], func=ACT.Sigmoid,
                    bias=per_feature(VB4, n)[:, c : c + 1],
                )
            return gate

        r_ps = [keep_ps.tile([P, PAIRS, P], F32, name="r_ps_%d" % n) for n in range(VARS)]

        def flat(rows_view):
            return rows_view.rearrange("p j q -> p (j q)")

        def x_into_rows(n):
            nc.tensor.matmul(out=flat(r_ps[n][:]), lhsT=ident_bf[:], rhs=flat(x_rows[:, n]), start=True, stop=False)

        gvs = [keep.tile([P, CHUNKS, BATCH], F32, name="gv_%d" % n) for n in range(VARS)]

        def gated_value(value_acc, gate, n, j):
            for c in (HALVES * j, HALVES * j + 1):
                nc.vector.scalar_tensor_tensor(
                    out=gvs[n][:, c, :], in0=value_acc[:, c, :], scalar=per_feature(VB5, n)[:, c : c + 1],
                    in1=gate[:, c, :], op0=ALU.add, op1=ALU.mult,
                )

        def add_rows(n, j, last):
            nc.tensor.matmul(
                out=r_ps[n][:, j, :],
                lhsT=gvs[n][:, j * HALVES : (j + 1) * HALVES, :].rearrange("p h b -> p (h b)"),
                rhs=ident_f[:], is_transpose=True, start=False, stop=last,
            )

        own = keep.tile([P, VARS, 2], F32)
        stats = {}

        def row_stats(n):
            stats[n] = keep.tile([P, 6], F32, name="stats_%d" % n)
            nc.vector.bn_stats(out=stats[n][:], in_=flat(r_ps[n][:]))

        def row_aggr(n):
            nc.vector.bn_aggr(out=own[:, n, :], in_=stats[n][:])

        dev = keep.tile([P, VARS], F32)
        rstd = keep.tile([P, VARS], F32)

        rows = {}

        def open_row(n, pool, tag):
            rows[n] = pool.tile([P, 2], F32, name="row_%d" % n, tag=tag)
            nc.tensor.matmul(out=rows[n][:], lhsT=pair[:], rhs=eps_cols[:, n, :], start=True, stop=False)

        def whole_row(n):
            nc.tensor.matmul(out=rows[n][:], lhsT=pair[:], rhs=own[:, n, :], start=False, stop=True)

        def one_over_std(n):
            col = slice(n, n + 1)
            nc.scalar.activation(out=dev[:, col], in_=rows[n][:, 0:1], func=ACT.Square, scale=-1.0, bias=own[:, n, 0:1])
            nc.scalar.activation(out=rstd[:, col], in_=rows[n][:, 1:2], func=ACT.Abs_reciprocal_sqrt, bias=dev[:, col])

        sel_gain = keep.tile([P, VARS, PAIRS * P], F32)
        sel_shift = keep.tile([P, VARS, PAIRS * P], F32)
        shift_sum = keep.tile([P, PAIRS * P], F32)

        def selection_times(target, spread):
            nc.gpsimd.tensor_tensor(
                out=target[:].rearrange("p n f -> p (n f)"), in0=sel_rows[:].rearrange("p n j q -> p (n j q)"),
                in1=spread[:].rearrange("p n j q -> p (n j q)"), op=ALU.mult,
            )

        def centred_times_gain(n):
            weighted = keep.tile([P, PAIRS * P], F32, name="weighted_%d" % n)
            nc.vector.scalar_tensor_tensor(
                out=weighted[:], in0=flat(r_ps[n][:]), scalar=rows[n][:, 0:1], in1=sel_gain[:, n, :],
                op0=ALU.subtract, op1=ALU.mult,
            )
            return weighted

        def scaled_plus(weighted, addend, n):
            summed = keep.tile([P, PAIRS * P], F32, name="summed_%d" % n)
            nc.vector.scalar_tensor_tensor(
                out=summed[:], in0=weighted[:], scalar=rstd[:, n : n + 1], in1=addend, op0=ALU.mult, op1=ALU.add
            )
            return summed[:]

        regroup("w1_1")
        quantise("w1_0")
        product("w1_0", hv_codes, hv_scales, 0, acc=e1_acc[:, 0])

        regroup("w4_0")
        quantise("w1_1")
        product("w1_1", hv_codes, hv_scales, 1, acc=e1_acc[:, 1])
        transpose_vectors()
        open_row(0, short_ps, "short")
        open_row(1, keep_ps, "row_1")

        regroup("w4_1")
        quantise("w4_0")
        e1_add()

        copy_vectors()
        regroup("w5_0")
        e1_quantise()
        gate_acc_0 = product("w4_0", e1_codes, e1_scales, 0)
        quantise("w4_1")
        gate_acc_1 = product("w4_1", e1_codes, e1_scales, 1)
        for n in range(VARS):
            x_into_rows(n)

        regroup("w5_1")
        quantise("w5_0")
        value_acc_0 = product("w5_0", e1_codes, e1_scales, 0)
        gate_0 = sigmoid(gate_acc_0, 0)
        gate_1 = sigmoid(gate_acc_1, 1)
        nc.scalar.activation(out=warm[:, 1:2], in_=one[:], func=ACT.Abs_reciprocal_sqrt)
        quantise("w5_1", 256, 512)
        value_acc_1b = product("w5_1", e1_codes, e1_scales, 1, (2, 3))
        quantise("w5_1", 0, 256)
        value_acc_1a = product("w5_1", e1_codes, e1_scales, 1, (0, 1))
        nc.vector.tensor_copy(out=sel_rows[:, 0, 0, 0:1], in_=sel_rows[:, 0, 0, 0:1])
        selection_times(sel_gain, gain_spread)
        selection_times(sel_shift, shift_spread)
        nc.gpsimd.tensor_tensor(out=shift_sum[:], in0=sel_shift[:, 0, :], in1=sel_shift[:, 1, :], op=ALU.add)

        gated_value(value_acc_0, gate_0, 0, 0)
        add_rows(0, 0, False)
        gated_value(value_acc_0, gate_0, 0, 1)
        add_rows(0, 1, True)
        gated_value(value_acc_1b, gate_1, 1, 1)
        add_rows(1, 1, False)
        gated_value(value_acc_1a, gate_1, 1, 0)
        add_rows(1, 0, True)
        row_stats(0)
        row_aggr(0)
        whole_row(0)
        row_stats(1)
        row_aggr(1)
        whole_row(1)
        one_over_std(0)
        one_over_std(1)
        weighted_0 = centred_times_gain(0)
        weighted_1 = centred_times_gain(1)
        total_0 = scaled_plus(weighted_0, shift_sum[:], 0)
        total = scaled_plus(weighted_1, total_0, 1)

        out_halves = out.rearrange("b (j h q) -> h b j q", h=HALVES, q=P)
        result = total.rearrange("p (j q) -> p j q", q=P)
        nc.sync.dma_start(out=out_halves[0], in_=result[:BATCH])
        nc.sync.dma_start(out=out_halves[1], in_=result[BATCH:])
